import numpy as np
import ml_dtypes


def mxq(x, axis, fmt="e4m3"):
    dtype, down = {"e4m3": (ml_dtypes.float8_e4m3fn, 7), "e5m2": (ml_dtypes.float8_e5m2, 14)}[fmt]
    v = np.moveaxis(np.asarray(x, np.float32).astype(ml_dtypes.bfloat16).astype(np.float64), axis, -1)
    blocks = v.reshape(v.shape[:-1] + (-1, 32))
    amax = np.abs(blocks).max(-1, keepdims=True)
    byte = np.maximum(np.where(amax > 0, np.frexp(amax)[1] - 1 + 127, 0) - down, 1)
    scale = np.exp2(byte - 127.0)
    codes = (blocks / scale).astype(np.float32).astype(dtype).astype(np.float64)
    return np.moveaxis((codes * scale).reshape(v.shape), -1, axis)


WIDE = False


def mx_kscale(k):
    if not WIDE:
        return np.ones(k)
    levels = np.array([10, -10, 5, -5, 0])
    a = np.random.permutation(np.resize(levels, k // 512 * 4)).reshape(k // 512, 4)
    idx = np.arange(k)
    return np.exp2(a[idx // 512, idx % 128 // 32])


BF16 = ml_dtypes.bfloat16


def bf(x):
    return np.asarray(x, np.float32).astype(BF16)


def f64(x):
    return np.asarray(x).astype(np.float64)


B, N, ATTR, STATE, REL, G, NF = 4, 32, 4, 16, 9, 32, 1024


def setup_inputs():
    rn = np.random.standard_normal
    s, u, t = mx_kscale(NF), mx_kscale(NF), mx_kscale(NF)
    rp_rows = np.concatenate([s, u, u])
    pp_rows = np.concatenate([u, t])
    pp_scale = np.concatenate([np.full(NF, 1.0 / np.sqrt(NF)), np.full(NF, 1.0 / np.sqrt(NF * N))])
    return {
        "rel_enc": bf(np.maximum(rn((B, N, N, NF)) * 1.1, 0.0) * s),
        "obj": bf(np.maximum(rn((B, N, NF)) * 1.1, 0.0) * u),
        "rp_w": bf(rn((3 * NF, NF)) * 2.0 / np.sqrt(3 * NF * N) / rp_rows[:, None] * t),
        "rp_b": bf(rn(NF) * 0.1 * t),
        "pp_w": bf(rn((2 * NF, NF)) * (pp_scale / pp_rows)[:, None]),
        "pp_b": bf(rn(NF) * 0.1),
    }


def reference(rel_enc, obj, rp_w, rp_b, pp_w, pp_b):
    rp, pp = f64(rp_w), f64(pp_w)
    oq = mxq(f64(obj), 2, "e4m3")
    e_rel = mxq(f64(rel_enc), 3, "e4m3") @ mxq(rp[:NF], 0, "e4m3")
    e_recv = oq @ mxq(rp[NF:2 * NF], 0, "e4m3")
    e_send = oq @ mxq(rp[2 * NF:], 0, "e4m3")
    rel_eff = np.maximum(e_rel + e_recv[:, :, None, :] + e_send[:, None, :, :] + f64(rp_b), 0.0)
    agg = rel_eff.sum(axis=2)
    p_obj = oq @ mxq(pp[:NF], 0, "e4m3")
    p_agg = mxq(agg, 2, "e4m3") @ mxq(pp[NF:], 0, "e4m3")
    return np.maximum(p_obj + p_agg + f64(pp_b), 0.0)

@@ -1,0 +1,284 @@
+from contextlib import ExitStack
+
+import concourse.mybir as mybir
+from concourse.masks import make_identity
+
+F32 = mybir.dt.float32
+BF16 = mybir.dt.bfloat16
+U32 = mybir.dt.uint32
+U8 = mybir.dt.uint8
+FP8X4 = mybir.dt.float8_e4m3fn_x4
+ADD = mybir.AluOpType.add
+RELU = mybir.ActivationFunctionType.Relu
+
+P = 128
+PACK = 4
+K_PASS = P * PACK
+BANK = 512
+GRAPHS = 4
+NODES = 32
+NF = 1024
+PASSES = NF // K_PASS
+F_TILES = NF // P
+HALVES = NF // BANK
+TILES_PER_HALF = BANK // P
+CHUNK_RECEIVERS = BANK // NODES
+CHUNKS = GRAPHS * NODES // CHUNK_RECEIVERS
+ROW_TILES = BANK // P
+
+FLOPS = 2 * (GRAPHS * NODES * NODES + 4 * GRAPHS * NODES) * NF * NF
+
+
+def tile_compositionalkoopmanoperators_pa_kernel(
+    tc, rel_enc, obj, rp_w, rp_b, pp_w, pp_b, out
+):
+    nc = tc.nc
+    relations = rel_enc.rearrange("b i j k -> (b i j) k")
+    particles = obj.rearrange("b i k -> (b i) k")
+    out_rows = out.rearrange("b i f -> (b i) f")
+    weight_rows = {
+        "wr": rp_w[0:NF, :],
+        "wi": rp_w[NF : 2 * NF, :],
+        "wj": rp_w[2 * NF : 3 * NF, :],
+        "po": pp_w[0:NF, :],
+        "pa": pp_w[NF : 2 * NF, :],
+    }
+
+    with ExitStack() as ctx:
+        ctx.enter_context(tc.manual_schedule())
+        const = ctx.enter_context(tc.tile_pool(name="const", bufs=1))
+        keep = ctx.enter_context(tc.tile_pool(name="keep", bufs=1))
+        w_raw_pool = ctx.enter_context(tc.tile_pool(name="w_raw", bufs=6))
+        w_grouped_pool = ctx.enter_context(tc.tile_pool(name="w_grouped", bufs=3))
+        x_raw_pool = ctx.enter_context(tc.tile_pool(name="x_raw", bufs=3))
+        x_pool = ctx.enter_context(tc.tile_pool(name="x", bufs=2))
+        pre_pool = ctx.enter_context(tc.tile_pool(name="pre", bufs=6))
+        result_pool = ctx.enter_context(tc.tile_pool(name="result", bufs=2))
+        psum_t = ctx.enter_context(tc.psum_pool(name="psum_t", bufs=2))
+        psum_e = ctx.enter_context(tc.psum_pool(name="psum_e", bufs=4))
+        psum_m = ctx.enter_context(tc.psum_pool(name="psum_m", bufs=2))
+
+        w_codes = {}
+        w_scales = {}
+        for weight in weight_rows:
+            w_codes[weight] = keep.tile(
+                [P, PASSES, NF], U32, name="%s_codes" % weight, align_bytes=64
+            )
+            w_scales[weight] = keep.tile(
+                [P, PASSES, NF], U8, name="%s_scales" % weight, align_bytes=64
+            )
+
+        ident = const.tile([P, P], F32)
+        make_identity(nc, ident[:])
+        ident_bf = const.tile([P, P], BF16)
+        nc.vector.tensor_copy(out=ident_bf[:], in_=ident[:])
+
+        def quantise_weight_piece(weight, g, h, regroup):
+            cols = slice(BANK * h, BANK * (h + 1))
+            rows = weight_rows[weight][K_PASS * g : K_PASS * (g + 1), cols]
+            raw = w_raw_pool.tile([P, PACK, BANK], BF16)
+            if weight == "pa":
+                nc.sync.dma_start(out=raw[:], in_=rows.rearrange("(t p) c -> p t c", p=P))
+            else:
+                for u in range(2):
+                    nc.sync.dma_start(
+                        out=raw[:, 2 * u : 2 * u + 2, :],
+                        in_=rows[2 * P * u : 2 * P * (u + 1), :].rearrange(
+                            "(p e) c -> p e c", e=2
+                        ),
+                    )
+            grouped = w_grouped_pool.tile([P, BANK, PACK], BF16, align_bytes=64)
+            regroup(
+                out=grouped[:].rearrange("p (c i) t -> p c t i", i=4),
+                in_=raw[:].rearrange("p t (c i) -> p c t i", i=4),
+            )
+            nc.vector.quantize_mx(
+                out=w_codes[weight][:, g, cols].bitcast(FP8X4),
+                scales=w_scales[weight][:, g, cols],
+                in_=grouped[:].rearrange("p c t -> p (c t)"),
+            )
+
+        x_codes = {}
+        x_scales = {}
+
+        def prepare_chunk(c, copy_out):
+            x_raw = x_raw_pool.tile([P, ROW_TILES, NF], BF16)
+            nc.sync.dma_start(
+                out=x_raw[:],
+                in_=relations[BANK * c : BANK * (c + 1), :].rearrange("(r p) k -> p r k", p=P),
+            )
+            x_grouped = x_pool.tile([P, PASSES, PACK * BANK], BF16, align_bytes=64)
+            codes = x_pool.tile([P, PASSES, BANK], U32, align_bytes=64)
+            scales = x_pool.tile([P, PASSES, BANK], U8, align_bytes=64)
+            for g in range(PASSES):
+                words_out = x_grouped[:, g, :].bitcast(F32).rearrange("p (c u) -> p c u", u=2)
+                for pair in range(ROW_TILES // 2):
+                    xt = psum_t.tile([P, 2, 2 * P], F32)
+                    for u in range(2):
+                        for r in range(2):
+                            words_in = x_raw[:, 2 * pair + r, :].bitcast(F32)
+                            nc.tensor.transpose(
+                                xt[:, u, P * r : P * (r + 1)],
+                                words_in[:, P * (2 * g + u) : P * (2 * g + u + 1)],
+                                ident[:],
+                            )
+                    copy_out(
+                        out=words_out[:, 2 * P * pair : 2 * P * (pair + 1), :],
+                        in_=xt[:].rearrange("p u c -> p c u"),
+                    )
+            for g in range(PASSES):
+                nc.vector.quantize_mx(
+                    out=codes[:, g, :].bitcast(FP8X4),
+                    scales=scales[:, g, :],
+                    in_=x_grouped[:, g, :],
+                )
+            x_codes[c] = codes
+            x_scales[c] = scales
+
+        prepare_chunk(0, nc.scalar.copy)
+
+        obj_raw = const.tile([P, NF], BF16)
+        nc.sync.dma_start(out=obj_raw[:], in_=particles)
+        bias_rows = const.tile([P, P], BF16)
+        nc.vector.memset(bias_rows[:], 0.0)
+        nc.sync.dma_start(out=bias_rows[0:F_TILES, :], in_=rp_b.rearrange("(m p) -> m p", p=P))
+
+        obj_t = psum_m.tile([P, 2 * PASSES, P], F32, tag="misc")
+        for w in range(2 * PASSES):
+            nc.tensor.transpose(
+                obj_t[:, w, :], obj_raw[:].bitcast(F32)[:, P * w : P * (w + 1)], ident[:]
+            )
+        obj_grouped = const.tile([P, PASSES * P * PACK], BF16, align_bytes=64)
+        nc.scalar.copy(
+            out=obj_grouped[:].bitcast(F32).rearrange("p (g r u) -> p g r u", g=PASSES, u=2),
+            in_=obj_t[:].rearrange("p (g u) r -> p g r u", u=2),
+        )
+        obj_codes = const.tile([P, PASSES, P], U32, align_bytes=64)
+        obj_scales = const.tile([P, PASSES, P], U8, align_bytes=64)
+        nc.vector.quantize_mx(
+            out=obj_codes[:].rearrange("p g r -> p (g r)").bitcast(FP8X4),
+            scales=obj_scales[:].rearrange("p g r -> p (g r)"),
+            in_=obj_grouped[:],
+        )
+
+        bias_t = psum_m.tile([P, P], BF16, tag="misc")
+        nc.tensor.transpose(bias_t[:], bias_rows[:], ident_bf[:])
+        rp_bias = const.tile([P, F_TILES], F32)
+        nc.vector.tensor_copy(out=rp_bias[:], in_=bias_t[:, 0:F_TILES])
+
+        e_send = keep.tile([P, F_TILES, P], F32)
+        e_recv = keep.tile([P, F_TILES, P], F32)
+        agg = keep.tile([P, PASSES, P, PACK], F32)
+
+        def particle_terms(h):
+            tiles = slice(TILES_PER_HALF * h, TILES_PER_HALF * (h + 1))
+            for weight in ("wj", "wi"):
+                bank = psum_m.tile([P, TILES_PER_HALF, P], F32, tag="misc")
+                for q in range(TILES_PER_HALF):
+                    f_cols = slice(BANK * h + P * q, BANK * h + P * (q + 1))
+                    for g in range(PASSES):
+                        nc.tensor.matmul_mx(
+                            out=bank[:, q, :],
+                            lhsT=w_codes[weight][:, g, f_cols].bitcast(FP8X4),
+                            lhsT_scale=w_scales[weight][:, g, f_cols],
+                            rhs=obj_codes[:, g, :].bitcast(FP8X4),
+                            rhs_scale=obj_scales[:, g, :],
+                            start=(g == 0),
+                            stop=(g == PASSES - 1),
+                        )
+                if weight == "wj":
+                    nc.scalar.copy(out=e_send[:, tiles, :], in_=bank[:])
+                else:
+                    nc.vector.tensor_tensor(
+                        out=e_recv[:, tiles, :],
+                        in0=bank[:],
+                        in1=rp_bias[:, tiles].unsqueeze(2).to_broadcast([P, TILES_PER_HALF, P]),
+                        op=ADD,
+                    )
+
+        def relation_effects(c, h):
+            graph = c * CHUNK_RECEIVERS // NODES
+            first = c * CHUNK_RECEIVERS
+            for q in range(TILES_PER_HALF):
+                m = TILES_PER_HALF * h + q
+                f_cols = slice(P * m, P * (m + 1))
+                acc = psum_e.tile([P, BANK], F32)
+                for g in range(PASSES):
+                    nc.tensor.matmul_mx(
+                        out=acc[:],
+                        lhsT=w_codes["wr"][:, g, f_cols].bitcast(FP8X4),
+                        lhsT_scale=w_scales["wr"][:, g, f_cols],
+                        rhs=x_codes[c][:, g, :].bitcast(FP8X4),
+                        rhs_scale=x_scales[c][:, g, :],
+                        start=(g == 0),
+                        stop=(g == PASSES - 1),
+                    )
+                pre = pre_pool.tile([P, CHUNK_RECEIVERS, NODES], F32)
+                nc.vector.tensor_tensor(
+                    out=pre[:],
+                    in0=acc[:].rearrange("p (i j) -> p i j", j=NODES),
+                    in1=e_send[:, m, NODES * graph : NODES * (graph + 1)]
+                    .unsqueeze(1)
+                    .to_broadcast([P, CHUNK_RECEIVERS, NODES]),
+                    op=ADD,
+                )
+                for i in range(CHUNK_RECEIVERS):
+                    nc.scalar.activation(
+                        out=pre[:, i, :],
+                        in_=pre[:, i, :],
+                        func=RELU,
+                        bias=e_recv[:, m, first + i : first + i + 1],
+                        accum_out=agg[:, m // PACK, first + i, m % PACK : m % PACK + 1],
+                    )
+
+        late_pieces = [
+            (weight, g, h) for weight in ("po", "pa") for h in range(HALVES) for g in range(PASSES)
+        ]
+        for c in range(CHUNKS):
+            for h in range(HALVES):
+                if c == 0:
+                    for weight in ("wr", "wj", "wi"):
+                        for g in range(PASSES):
+                            idle_scalar = h == 0 and g == 1
+                            quantise_weight_piece(
+                                weight, g, h, nc.scalar.copy if idle_scalar else nc.vector.tensor_copy
+                            )
+                    particle_terms(h)
+                if h == HALVES - 1:
+                    if c + 1 < CHUNKS:
+                        prepare_chunk(c + 1, nc.vector.tensor_copy)
+                    weight, g, piece_half = late_pieces[c]
+                    quantise_weight_piece(weight, g, piece_half, nc.vector.tensor_copy)
+                relation_effects(c, h)
+
+        pp_bias = const.tile([P, NF], BF16)
+        nc.sync.dma_start(out=pp_bias[:], in_=pp_b.partition_broadcast(P))
+
+        agg_bf = const.tile([P, PASSES * P * PACK], BF16, align_bytes=64)
+        nc.vector.tensor_copy(out=agg_bf[:], in_=agg[:].rearrange("p g r t -> p (g r t)"))
+        agg_codes = const.tile([P, PASSES, P], U32, align_bytes=64)
+        agg_scales = const.tile([P, PASSES, P], U8, align_bytes=64)
+        nc.vector.quantize_mx(
+            out=agg_codes[:].rearrange("p g r -> p (g r)").bitcast(FP8X4),
+            scales=agg_scales[:].rearrange("p g r -> p (g r)"),
+            in_=agg_bf[:],
+        )
+        for h in range(HALVES):
+            cols = slice(BANK * h, BANK * (h + 1))
+            total = psum_m.tile([P, BANK], F32, tag="misc")
+            products = (("po", obj_codes, obj_scales), ("pa", agg_codes, agg_scales))
+            for n, (weight, codes, scales) in enumerate(products):
+                for g in range(PASSES):
+                    nc.tensor.matmul_mx(
+                        out=total[:],
+                        lhsT=codes[:, g, :].bitcast(FP8X4),
+                        lhsT_scale=scales[:, g, :],
+                        rhs=w_codes[weight][:, g, cols].bitcast(FP8X4),
+                        rhs_scale=w_scales[weight][:, g, cols],
+                        start=(n == 0 and g == 0),
+                        stop=(n == 1 and g == PASSES - 1),
+                    )
+            result = result_pool.tile([P, BANK], F32)
+            nc.vector.tensor_tensor(out=result[:], in0=total[:], in1=pp_bias[:, cols], op=ADD)
+            nc.scalar.activation(out=result[:], in_=result[:], func=RELU)
+            nc.sync.dma_start(out=out_rows[:, cols], in_=result[:])

@@ -7,8 +7,12 @@ F32 = mybir.dt.float32
 BF16 = mybir.dt.bfloat16
 U32 = mybir.dt.uint32
 U8 = mybir.dt.uint8
+I32 = mybir.dt.int32
 FP8X4 = mybir.dt.float8_e4m3fn_x4
 ADD = mybir.AluOpType.add
+SUBTRACT = mybir.AluOpType.subtract
+MULT = mybir.AluOpType.mult
+MAX = mybir.AluOpType.max
 RELU = mybir.ActivationFunctionType.Relu
 
 P = 128
@@ -52,11 +56,11 @@ def tile_compositionalkoopmanoperators_pa_kernel(
         w_grouped_pool = ctx.enter_context(tc.tile_pool(name="w_grouped", bufs=3))
         x_raw_pool = ctx.enter_context(tc.tile_pool(name="x_raw", bufs=3))
         x_pool = ctx.enter_context(tc.tile_pool(name="x", bufs=2))
-        pre_pool = ctx.enter_context(tc.tile_pool(name="pre", bufs=6))
+        send_pool = ctx.enter_context(tc.tile_pool(name="send", bufs=2))
+        clip_pool = ctx.enter_context(tc.tile_pool(name="clip", bufs=4))
         result_pool = ctx.enter_context(tc.tile_pool(name="result", bufs=2))
         psum_t = ctx.enter_context(tc.psum_pool(name="psum_t", bufs=2))
-        psum_e = ctx.enter_context(tc.psum_pool(name="psum_e", bufs=4))
-        psum_m = ctx.enter_context(tc.psum_pool(name="psum_m", bufs=2))
+        psum_e = ctx.enter_context(tc.psum_pool(name="psum_e", bufs=6))
 
         w_codes = {}
         w_scales = {}
@@ -101,7 +105,31 @@ def tile_compositionalkoopmanoperators_pa_kernel(
         x_codes = {}
         x_scales = {}
 
-        def prepare_chunk(c, copy_out):
+        send_codes = {}
+        send_scales = {}
+
+        def repeat_senders(graph):
+            senders = slice(NODES * graph, NODES * (graph + 1))
+            rep_codes = send_pool.tile([P, PASSES, BANK], U32, align_bytes=64)
+            rep_scales = send_pool.tile([P, PASSES, BANK], U8, align_bytes=64)
+            nc.vector.tensor_copy(
+                out=rep_codes[:].bitcast(I32).rearrange("p g (i j) -> p g i j", j=NODES),
+                in_=obj_codes[:, :, senders]
+                .bitcast(I32)
+                .unsqueeze(2)
+                .to_broadcast([P, PASSES, CHUNK_RECEIVERS, NODES]),
+            )
+            nc.vector.tensor_copy(
+                out=rep_scales[:].bitcast(I32).rearrange("p g (i w) -> p g i w", w=NODES // 4),
+                in_=obj_scales[:, :, senders]
+                .bitcast(I32)
+                .unsqueeze(2)
+                .to_broadcast([P, PASSES, CHUNK_RECEIVERS, NODES // 4]),
+            )
+            send_codes[graph] = rep_codes
+            send_scales[graph] = rep_scales
+
+        def prepare_chunk(c):
             x_raw = x_raw_pool.tile([P, ROW_TILES, NF], BF16)
             nc.sync.dma_start(
                 out=x_raw[:],
@@ -113,7 +141,7 @@ def tile_compositionalkoopmanoperators_pa_kernel(
             for g in range(PASSES):
                 words_out = x_grouped[:, g, :].bitcast(F32).rearrange("p (c u) -> p c u", u=2)
                 for pair in range(ROW_TILES // 2):
-                    xt = psum_t.tile([P, 2, 2 * P], F32)
+                    xt = psum_t.tile([P, 2, 2 * P], F32, tag="small")
                     for u in range(2):
                         for r in range(2):
                             words_in = x_raw[:, 2 * pair + r, :].bitcast(F32)
@@ -122,7 +150,7 @@ def tile_compositionalkoopmanoperators_pa_kernel(
                                 words_in[:, P * (2 * g + u) : P * (2 * g + u + 1)],
                                 ident[:],
                             )
-                    copy_out(
+                    nc.scalar.copy(
                         out=words_out[:, 2 * P * pair : 2 * P * (pair + 1), :],
                         in_=xt[:].rearrange("p u c -> p c u"),
                     )
@@ -135,7 +163,7 @@ def tile_compositionalkoopmanoperators_pa_kernel(
             x_codes[c] = codes
             x_scales[c] = scales
 
-        prepare_chunk(0, nc.scalar.copy)
+        prepare_chunk(0)
 
         obj_raw = const.tile([P, NF], BF16)
         nc.sync.dma_start(out=obj_raw[:], in_=particles)
@@ -143,7 +171,7 @@ def tile_compositionalkoopmanoperators_pa_kernel(
         nc.vector.memset(bias_rows[:], 0.0)
         nc.sync.dma_start(out=bias_rows[0:F_TILES, :], in_=rp_b.rearrange("(m p) -> m p", p=P))
 
-        obj_t = psum_m.tile([P, 2 * PASSES, P], F32, tag="misc")
+        obj_t = psum_t.tile([P, 2 * PASSES, P], F32, tag="small")
         for w in range(2 * PASSES):
             nc.tensor.transpose(
                 obj_t[:, w, :], obj_raw[:].bitcast(F32)[:, P * w : P * (w + 1)], ident[:]
@@ -155,80 +183,83 @@ def tile_compositionalkoopmanoperators_pa_kernel(
         )
         obj_codes = const.tile([P, PASSES, P], U32, align_bytes=64)
         obj_scales = const.tile([P, PASSES, P], U8, align_bytes=64)
+        nc.vector.memset(obj_scales[:].bitcast(I32), 0)
         nc.vector.quantize_mx(
             out=obj_codes[:].rearrange("p g r -> p (g r)").bitcast(FP8X4),
             scales=obj_scales[:].rearrange("p g r -> p (g r)"),
             in_=obj_grouped[:],
         )
 
-        bias_t = psum_m.tile([P, P], BF16, tag="misc")
+        bias_t = psum_t.tile([P, P], BF16, tag="small")
         nc.tensor.transpose(bias_t[:], bias_rows[:], ident_bf[:])
-        rp_bias = const.tile([P, F_TILES], F32)
-        nc.vector.tensor_copy(out=rp_bias[:], in_=bias_t[:, 0:F_TILES])
+        neg_rp_bias = const.tile([P, F_TILES], F32)
+        nc.vector.tensor_scalar_mul(out=neg_rp_bias[:], in0=bias_t[:, 0:F_TILES], scalar1=-1.0)
+        repeat_senders(0)
 
-        e_send = keep.tile([P, F_TILES, P], F32)
-        e_recv = keep.tile([P, F_TILES, P], F32)
+        neg_recv = keep.tile([P, PASSES, P, PACK], F32)
         agg = keep.tile([P, PASSES, P, PACK], F32)
 
-        def particle_terms(h):
+        def receiver_terms(h):
             tiles = slice(TILES_PER_HALF * h, TILES_PER_HALF * (h + 1))
-            for weight in ("wj", "wi"):
-                bank = psum_m.tile([P, TILES_PER_HALF, P], F32, tag="misc")
-                for q in range(TILES_PER_HALF):
-                    f_cols = slice(BANK * h + P * q, BANK * h + P * (q + 1))
-                    for g in range(PASSES):
-                        nc.tensor.matmul_mx(
-                            out=bank[:, q, :],
-                            lhsT=w_codes[weight][:, g, f_cols].bitcast(FP8X4),
-                            lhsT_scale=w_scales[weight][:, g, f_cols],
-                            rhs=obj_codes[:, g, :].bitcast(FP8X4),
-                            rhs_scale=obj_scales[:, g, :],
-                            start=(g == 0),
-                            stop=(g == PASSES - 1),
-                        )
-                if weight == "wj":
-                    nc.scalar.copy(out=e_send[:, tiles, :], in_=bank[:])
-                else:
-                    nc.vector.tensor_tensor(
-                        out=e_recv[:, tiles, :],
-                        in0=bank[:],
-                        in1=rp_bias[:, tiles].unsqueeze(2).to_broadcast([P, TILES_PER_HALF, P]),
-                        op=ADD,
-                    )
-
-        def relation_effects(c, h):
-            graph = c * CHUNK_RECEIVERS // NODES
-            first = c * CHUNK_RECEIVERS
+            bank = psum_t.tile([P, TILES_PER_HALF, P], F32, tag="small")
             for q in range(TILES_PER_HALF):
-                m = TILES_PER_HALF * h + q
-                f_cols = slice(P * m, P * (m + 1))
-                acc = psum_e.tile([P, BANK], F32)
+                f_cols = slice(BANK * h + P * q, BANK * h + P * (q + 1))
                 for g in range(PASSES):
                     nc.tensor.matmul_mx(
-                        out=acc[:],
-                        lhsT=w_codes["wr"][:, g, f_cols].bitcast(FP8X4),
-                        lhsT_scale=w_scales["wr"][:, g, f_cols],
-                        rhs=x_codes[c][:, g, :].bitcast(FP8X4),
-                        rhs_scale=x_scales[c][:, g, :],
+                        out=bank[:, q, :],
+                        lhsT=w_codes["wi"][:, g, f_cols].bitcast(FP8X4),
+                        lhsT_scale=w_scales["wi"][:, g, f_cols],
+                        rhs=obj_codes[:, g, :].bitcast(FP8X4),
+                        rhs_scale=obj_scales[:, g, :],
                         start=(g == 0),
                         stop=(g == PASSES - 1),
                     )
-                pre = pre_pool.tile([P, CHUNK_RECEIVERS, NODES], F32)
-                nc.vector.tensor_tensor(
-                    out=pre[:],
-                    in0=acc[:].rearrange("p (i j) -> p i j", j=NODES),
-                    in1=e_send[:, m, NODES * graph : NODES * (graph + 1)]
-                    .unsqueeze(1)
-                    .to_broadcast([P, CHUNK_RECEIVERS, NODES]),
-                    op=ADD,
-                )
-                for i in range(CHUNK_RECEIVERS):
-                    nc.scalar.activation(
-                        out=pre[:, i, :],
-                        in_=pre[:, i, :],
-                        func=RELU,
-                        bias=e_recv[:, m, first + i : first + i + 1],
-                        accum_out=agg[:, m // PACK, first + i, m % PACK : m % PACK + 1],
+            nc.vector.tensor_tensor(
+                out=neg_recv[:, h, :, :],
+                in0=neg_rp_bias[:, tiles].unsqueeze(1).to_broadcast([P, P, TILES_PER_HALF]),
+                in1=bank[:].rearrange("p q r -> p r q"),
+                op=SUBTRACT,
+            )
+
+        def relation_effects(c, h):
+            graph = c * CHUNK_RECEIVERS // NODES
+            receivers = slice(c * CHUNK_RECEIVERS, (c + 1) * CHUNK_RECEIVERS)
+            operands = (
+                ("wr", x_codes[c], x_scales[c]),
+                ("wj", send_codes[graph], send_scales[graph]),
+            )
+            clipped_tiles = {}
+            for q in range(TILES_PER_HALF + 1):
+                if q < TILES_PER_HALF:
+                    f_cols = slice(BANK * h + P * q, BANK * h + P * (q + 1))
+                    acc = psum_e.tile([P, BANK], F32)
+                    for n, (weight, codes, scales) in enumerate(operands):
+                        for g in range(PASSES):
+                            nc.tensor.matmul_mx(
+                                out=acc[:],
+                                lhsT=w_codes[weight][:, g, f_cols].bitcast(FP8X4),
+                                lhsT_scale=w_scales[weight][:, g, f_cols],
+                                rhs=codes[:, g, :].bitcast(FP8X4),
+                                rhs_scale=scales[:, g, :],
+                                start=(n == 0 and g == 0),
+                                stop=(n == 1 and g == PASSES - 1),
+                            )
+                    clipped = clip_pool.tile([P, CHUNK_RECEIVERS, NODES], F32)
+                    nc.vector.tensor_tensor(
+                        out=clipped[:],
+                        in0=acc[:].rearrange("p (i j) -> p i j", j=NODES),
+                        in1=neg_recv[:, h, receivers, q]
+                        .unsqueeze(2)
+                        .to_broadcast([P, CHUNK_RECEIVERS, NODES]),
+                        op=MAX,
+                    )
+                    clipped_tiles[q] = clipped
+                if q > 0:
+                    nc.vector.tensor_reduce(
+                        out=agg[:, h, receivers, q - 1],
+                        in_=clipped_tiles[q - 1][:],
+                        axis=mybir.AxisListType.X,
+                        op=ADD,
                     )
 
         late_pieces = [
@@ -239,23 +270,31 @@ def tile_compositionalkoopmanoperators_pa_kernel(
                 if c == 0:
                     for weight in ("wr", "wj", "wi"):
                         for g in range(PASSES):
-                            idle_scalar = h == 0 and g == 1
                             quantise_weight_piece(
-                                weight, g, h, nc.scalar.copy if idle_scalar else nc.vector.tensor_copy
+                                weight, g, h, nc.vector.tensor_copy if g == 0 else nc.scalar.copy
                             )
-                    particle_terms(h)
+                    receiver_terms(h)
                 if h == HALVES - 1:
                     if c + 1 < CHUNKS:
-                        prepare_chunk(c + 1, nc.vector.tensor_copy)
+                        prepare_chunk(c + 1)
+                        if (c + 1) * CHUNK_RECEIVERS % NODES == 0:
+                            repeat_senders((c + 1) * CHUNK_RECEIVERS // NODES)
                     weight, g, piece_half = late_pieces[c]
-                    quantise_weight_piece(weight, g, piece_half, nc.vector.tensor_copy)
+                    quantise_weight_piece(weight, g, piece_half, nc.scalar.copy)
                 relation_effects(c, h)
 
         pp_bias = const.tile([P, NF], BF16)
         nc.sync.dma_start(out=pp_bias[:], in_=pp_b.partition_broadcast(P))
 
         agg_bf = const.tile([P, PASSES * P * PACK], BF16, align_bytes=64)
-        nc.vector.tensor_copy(out=agg_bf[:], in_=agg[:].rearrange("p g r t -> p (g r t)"))
+        nc.vector.scalar_tensor_tensor(
+            out=agg_bf[:],
+            in0=neg_recv[:].rearrange("p g r t -> p (g r t)"),
+            scalar=-float(NODES),
+            in1=agg[:].rearrange("p g r t -> p (g r t)"),
+            op0=MULT,
+            op1=ADD,
+        )
         agg_codes = const.tile([P, PASSES, P], U32, align_bytes=64)
         agg_scales = const.tile([P, PASSES, P], U8, align_bytes=64)
         nc.vector.quantize_mx(
@@ -265,7 +304,7 @@ def tile_compositionalkoopmanoperators_pa_kernel(
         )
         for h in range(HALVES):
             cols = slice(BANK * h, BANK * (h + 1))
-            total = psum_m.tile([P, BANK], F32, tag="misc")
+            total = psum_e.tile([P, BANK], F32, tag="acc")
             products = (("po", obj_codes, obj_scales), ("pa", agg_codes, agg_scales))
             for n, (weight, codes, scales) in enumerate(products):
                 for g in range(PASSES):

@@ -14,6 +14,7 @@ SUBTRACT = mybir.AluOpType.subtract
 MULT = mybir.AluOpType.mult
 MAX = mybir.AluOpType.max
 RELU = mybir.ActivationFunctionType.Relu
+IDENTITY = mybir.ActivationFunctionType.Identity
 
 P = 128
 PACK = 4
@@ -29,6 +30,8 @@ TILES_PER_HALF = BANK // P
 CHUNK_RECEIVERS = BANK // NODES
 CHUNKS = GRAPHS * NODES // CHUNK_RECEIVERS
 ROW_TILES = BANK // P
+VECTOR_TILES = 3
+SUM_LAG = 2
 
 FLOPS = 2 * (GRAPHS * NODES * NODES + 4 * GRAPHS * NODES) * NF * NF
 
@@ -58,9 +61,10 @@ def tile_compositionalkoopmanoperators_pa_kernel(
         x_pool = ctx.enter_context(tc.tile_pool(name="x", bufs=2))
         send_pool = ctx.enter_context(tc.tile_pool(name="send", bufs=2))
         clip_pool = ctx.enter_context(tc.tile_pool(name="clip", bufs=4))
+        junk_pool = ctx.enter_context(tc.tile_pool(name="junk", bufs=2))
         result_pool = ctx.enter_context(tc.tile_pool(name="result", bufs=2))
-        psum_t = ctx.enter_context(tc.psum_pool(name="psum_t", bufs=2))
-        psum_e = ctx.enter_context(tc.psum_pool(name="psum_e", bufs=6))
+        psum_t = ctx.enter_context(tc.psum_pool(name="psum_t", bufs=4))
+        psum_e = ctx.enter_context(tc.psum_pool(name="psum_e", bufs=4))
 
         w_codes = {}
         w_scales = {}
@@ -102,11 +106,46 @@ def tile_compositionalkoopmanoperators_pa_kernel(
                 in_=grouped[:].rearrange("p c t -> p (c t)"),
             )
 
+        def early_weight(weight, h):
+            for g in range(PASSES):
+                quantise_weight_piece(
+                    weight, g, h, nc.vector.tensor_copy if g == 0 else nc.scalar.copy
+                )
+
+        x_grouped = {}
         x_codes = {}
         x_scales = {}
-
         send_codes = {}
         send_scales = {}
+
+        def transpose_chunk(c):
+            x_raw = x_raw_pool.tile([P, ROW_TILES, NF], BF16)
+            nc.sync.dma_start(
+                out=x_raw[:],
+                in_=relations[BANK * c : BANK * (c + 1), :].rearrange("(r p) k -> p r k", p=P),
+            )
+            grouped = x_pool.tile([P, PASSES, PACK * BANK], BF16, name="x_grouped", align_bytes=64)
+            banks = {}
+            for g in range(PASSES):
+                for pair in range(ROW_TILES // 2):
+                    xt = psum_t.tile([P, 2, 2 * P], F32, tag="small")
+                    for u in range(2):
+                        for r in range(2):
+                            words_in = x_raw[:, 2 * pair + r, :].bitcast(F32)
+                            nc.tensor.transpose(
+                                xt[:, u, P * r : P * (r + 1)],
+                                words_in[:, P * (2 * g + u) : P * (2 * g + u + 1)],
+                                ident[:],
+                            )
+                    banks[(g, pair)] = xt
+            for g in range(PASSES):
+                words_out = grouped[:, g, :].bitcast(F32).rearrange("p (c u) -> p c u", u=2)
+                for pair in range(ROW_TILES // 2):
+                    nc.scalar.copy(
+                        out=words_out[:, 2 * P * pair : 2 * P * (pair + 1), :],
+                        in_=banks[(g, pair)][:].rearrange("p u c -> p c u"),
+                    )
+            x_grouped[c] = grouped
 
         def repeat_senders(graph):
             senders = slice(NODES * graph, NODES * (graph + 1))
@@ -129,41 +168,21 @@ def tile_compositionalkoopmanoperators_pa_kernel(
             send_codes[graph] = rep_codes
             send_scales[graph] = rep_scales
 
-        def prepare_chunk(c):
-            x_raw = x_raw_pool.tile([P, ROW_TILES, NF], BF16)
-            nc.sync.dma_start(
-                out=x_raw[:],
-                in_=relations[BANK * c : BANK * (c + 1), :].rearrange("(r p) k -> p r k", p=P),
-            )
-            x_grouped = x_pool.tile([P, PASSES, PACK * BANK], BF16, align_bytes=64)
-            codes = x_pool.tile([P, PASSES, BANK], U32, align_bytes=64)
-            scales = x_pool.tile([P, PASSES, BANK], U8, align_bytes=64)
-            for g in range(PASSES):
-                words_out = x_grouped[:, g, :].bitcast(F32).rearrange("p (c u) -> p c u", u=2)
-                for pair in range(ROW_TILES // 2):
-                    xt = psum_t.tile([P, 2, 2 * P], F32, tag="small")
-                    for u in range(2):
-                        for r in range(2):
-                            words_in = x_raw[:, 2 * pair + r, :].bitcast(F32)
-                            nc.tensor.transpose(
-                                xt[:, u, P * r : P * (r + 1)],
-                                words_in[:, P * (2 * g + u) : P * (2 * g + u + 1)],
-                                ident[:],
-                            )
-                    nc.scalar.copy(
-                        out=words_out[:, 2 * P * pair : 2 * P * (pair + 1), :],
-                        in_=xt[:].rearrange("p u c -> p c u"),
-                    )
+        def quantise_chunk(c):
+            codes = x_pool.tile([P, PASSES, BANK], U32, name="x_codes", align_bytes=64)
+            scales = x_pool.tile([P, PASSES, BANK], U8, name="x_scales", align_bytes=64)
             for g in range(PASSES):
                 nc.vector.quantize_mx(
                     out=codes[:, g, :].bitcast(FP8X4),
                     scales=scales[:, g, :],
-                    in_=x_grouped[:, g, :],
+                    in_=x_grouped[c][:, g, :],
                 )
             x_codes[c] = codes
             x_scales[c] = scales
+            if c * CHUNK_RECEIVERS % NODES == 0:
+                repeat_senders(c * CHUNK_RECEIVERS // NODES)
 
-        prepare_chunk(0)
+        transpose_chunk(0)
 
         obj_raw = const.tile([P, NF], BF16)
         nc.sync.dma_start(out=obj_raw[:], in_=particles)
@@ -189,18 +208,22 @@ def tile_compositionalkoopmanoperators_pa_kernel(
             scales=obj_scales[:].rearrange("p g r -> p (g r)"),
             in_=obj_grouped[:],
         )
+        quantise_chunk(0)
 
         bias_t = psum_t.tile([P, P], BF16, tag="small")
         nc.tensor.transpose(bias_t[:], bias_rows[:], ident_bf[:])
+        rp_bias = const.tile([P, F_TILES], F32)
+        nc.vector.tensor_copy(out=rp_bias[:], in_=bias_t[:, 0:F_TILES])
         neg_rp_bias = const.tile([P, F_TILES], F32)
         nc.vector.tensor_scalar_mul(out=neg_rp_bias[:], in0=bias_t[:, 0:F_TILES], scalar1=-1.0)
-        repeat_senders(0)
 
-        neg_recv = keep.tile([P, PASSES, P, PACK], F32)
-        agg = keep.tile([P, PASSES, P, PACK], F32)
+        neg_recv = keep.tile([P, PASSES, P, VECTOR_TILES], F32)
+        clipped_sum = keep.tile([P, PASSES, P, VECTOR_TILES], F32)
+        scalar_recv = keep.tile([P, PASSES, P], F32)
+        scalar_agg = keep.tile([P, PASSES, P], F32)
 
         def receiver_terms(h):
-            tiles = slice(TILES_PER_HALF * h, TILES_PER_HALF * (h + 1))
+            first_tile = TILES_PER_HALF * h
             bank = psum_t.tile([P, TILES_PER_HALF, P], F32, tag="small")
             for q in range(TILES_PER_HALF):
                 f_cols = slice(BANK * h + P * q, BANK * h + P * (q + 1))
@@ -216,84 +239,124 @@ def tile_compositionalkoopmanoperators_pa_kernel(
                     )
             nc.vector.tensor_tensor(
                 out=neg_recv[:, h, :, :],
-                in0=neg_rp_bias[:, tiles].unsqueeze(1).to_broadcast([P, P, TILES_PER_HALF]),
-                in1=bank[:].rearrange("p q r -> p r q"),
+                in0=neg_rp_bias[:, first_tile : first_tile + VECTOR_TILES]
+                .unsqueeze(1)
+                .to_broadcast([P, P, VECTOR_TILES]),
+                in1=bank[:, 0:VECTOR_TILES, :].rearrange("p q r -> p r q"),
                 op=SUBTRACT,
             )
+            nc.scalar.activation(
+                out=scalar_recv[:, h, :],
+                in_=bank[:, VECTOR_TILES, :],
+                func=IDENTITY,
+                bias=rp_bias[:, first_tile + VECTOR_TILES : first_tile + VECTOR_TILES + 1],
+            )
 
-        def relation_effects(c, h):
+        def multiply_bank(c, h, q):
             graph = c * CHUNK_RECEIVERS // NODES
-            receivers = slice(c * CHUNK_RECEIVERS, (c + 1) * CHUNK_RECEIVERS)
             operands = (
                 ("wr", x_codes[c], x_scales[c]),
                 ("wj", send_codes[graph], send_scales[graph]),
             )
-            clipped_tiles = {}
-            for q in range(TILES_PER_HALF + 1):
-                if q < TILES_PER_HALF:
-                    f_cols = slice(BANK * h + P * q, BANK * h + P * (q + 1))
-                    acc = psum_e.tile([P, BANK], F32)
-                    for n, (weight, codes, scales) in enumerate(operands):
-                        for g in range(PASSES):
-                            nc.tensor.matmul_mx(
-                                out=acc[:],
-                                lhsT=w_codes[weight][:, g, f_cols].bitcast(FP8X4),
-                                lhsT_scale=w_scales[weight][:, g, f_cols],
-                                rhs=codes[:, g, :].bitcast(FP8X4),
-                                rhs_scale=scales[:, g, :],
-                                start=(n == 0 and g == 0),
-                                stop=(n == 1 and g == PASSES - 1),
-                            )
-                    clipped = clip_pool.tile([P, CHUNK_RECEIVERS, NODES], F32)
-                    nc.vector.tensor_tensor(
-                        out=clipped[:],
-                        in0=acc[:].rearrange("p (i j) -> p i j", j=NODES),
-                        in1=neg_recv[:, h, receivers, q]
-                        .unsqueeze(2)
-                        .to_broadcast([P, CHUNK_RECEIVERS, NODES]),
-                        op=MAX,
+            f_cols = slice(BANK * h + P * q, BANK * h + P * (q + 1))
+            acc = psum_e.tile([P, BANK], F32)
+            for n, (weight, codes, scales) in enumerate(operands):
+                for g in range(PASSES):
+                    nc.tensor.matmul_mx(
+                        out=acc[:],
+                        lhsT=w_codes[weight][:, g, f_cols].bitcast(FP8X4),
+                        lhsT_scale=w_scales[weight][:, g, f_cols],
+                        rhs=codes[:, g, :].bitcast(FP8X4),
+                        rhs_scale=scales[:, g, :],
+                        start=(n == 0 and g == 0),
+                        stop=(n == 1 and g == PASSES - 1),
                     )
-                    clipped_tiles[q] = clipped
-                if q > 0:
-                    nc.vector.tensor_reduce(
-                        out=agg[:, h, receivers, q - 1],
-                        in_=clipped_tiles[q - 1][:],
-                        axis=mybir.AxisListType.X,
-                        op=ADD,
-                    )
+            return acc[:].rearrange("p (i j) -> p i j", j=NODES)
+
+        def clip_and_fold(x, c, h, q):
+            receivers = slice(c * CHUNK_RECEIVERS, (c + 1) * CHUNK_RECEIVERS)
+            clipped = clip_pool.tile([P, CHUNK_RECEIVERS, NODES], F32)
+            nc.vector.tensor_tensor(
+                out=clipped[:],
+                in0=x,
+                in1=neg_recv[:, h, receivers, q]
+                .unsqueeze(2)
+                .to_broadcast([P, CHUNK_RECEIVERS, NODES]),
+                op=MAX,
+            )
+            folded = clip_pool.tile([P, CHUNK_RECEIVERS, NODES // 2], F32)
+            nc.gpsimd.tensor_tensor(
+                out=folded[:],
+                in0=clipped[:, :, 0 : NODES // 2],
+                in1=clipped[:, :, NODES // 2 : NODES],
+                op=ADD,
+            )
+            return folded, clipped_sum[:, h, receivers, q]
+
+        def sum_bank(folded, target):
+            nc.vector.tensor_reduce(out=target, in_=folded[:], axis=mybir.AxisListType.X, op=ADD)
+
+        def scalar_sums(x, c, h):
+            junk = junk_pool.tile([P, CHUNK_RECEIVERS, NODES], F32)
+            for i in range(CHUNK_RECEIVERS):
+                r = c * CHUNK_RECEIVERS + i
+                nc.scalar.activation(
+                    out=junk[:, i, :],
+                    in_=x[:, i, :],
+                    func=RELU,
+                    bias=scalar_recv[:, h, r : r + 1],
+                    accum_out=scalar_agg[:, h, r : r + 1],
+                )
+
+        def early_half(h):
+            early_weight("wi", h)
+            receiver_terms(h)
+            early_weight("wr", h)
+            early_weight("wj", h)
+
+        early_half(0)
+        transpose_chunk(1)
 
         late_pieces = [
             (weight, g, h) for weight in ("po", "pa") for h in range(HALVES) for g in range(PASSES)
         ]
+        folded_banks = []
         for c in range(CHUNKS):
             for h in range(HALVES):
-                if c == 0:
-                    for weight in ("wr", "wj", "wi"):
-                        for g in range(PASSES):
-                            quantise_weight_piece(
-                                weight, g, h, nc.vector.tensor_copy if g == 0 else nc.scalar.copy
-                            )
-                    receiver_terms(h)
-                if h == HALVES - 1:
+                for q in range(TILES_PER_HALF):
+                    x = multiply_bank(c, h, q)
+                    if q < VECTOR_TILES:
+                        folded_banks.append(clip_and_fold(x, c, h, q))
+                        if len(folded_banks) > SUM_LAG:
+                            sum_bank(*folded_banks[len(folded_banks) - 1 - SUM_LAG])
+                    else:
+                        scalar_sums(x, c, h)
+                if h == 0:
+                    if c == 0:
+                        early_half(1)
                     if c + 1 < CHUNKS:
-                        prepare_chunk(c + 1)
-                        if (c + 1) * CHUNK_RECEIVERS % NODES == 0:
-                            repeat_senders((c + 1) * CHUNK_RECEIVERS // NODES)
-                    weight, g, piece_half = late_pieces[c]
-                    quantise_weight_piece(weight, g, piece_half, nc.scalar.copy)
-                relation_effects(c, h)
+                        quantise_chunk(c + 1)
+                    if c + 2 < CHUNKS:
+                        transpose_chunk(c + 2)
+                    quantise_weight_piece(*late_pieces[c], nc.vector.tensor_copy)
+        for n in range(len(folded_banks) - SUM_LAG, len(folded_banks)):
+            sum_bank(*folded_banks[n])
 
         pp_bias = const.tile([P, NF], BF16)
         nc.sync.dma_start(out=pp_bias[:], in_=pp_b.partition_broadcast(P))
 
         agg_bf = const.tile([P, PASSES * P * PACK], BF16, align_bytes=64)
+        agg_words = agg_bf[:].rearrange("p (w t) -> p w t", t=PACK)
         nc.vector.scalar_tensor_tensor(
-            out=agg_bf[:],
-            in0=neg_recv[:].rearrange("p g r t -> p (g r t)"),
+            out=agg_words[:, :, 0:VECTOR_TILES],
+            in0=neg_recv[:].rearrange("p g r t -> p (g r) t"),
             scalar=-float(NODES),
-            in1=agg[:].rearrange("p g r t -> p (g r t)"),
+            in1=clipped_sum[:].rearrange("p g r t -> p (g r) t"),
             op0=MULT,
             op1=ADD,
+        )
+        nc.vector.tensor_copy(
+            out=agg_words[:, :, VECTOR_TILES], in_=scalar_agg[:].rearrange("p g r -> p (g r)")
         )
         agg_codes = const.tile([P, PASSES, P], U32, align_bytes=64)
         agg_scales = const.tile([P, PASSES, P], U8, align_bytes=64)

@@ -52,7 +52,6 @@ def tile_compositionalkoopmanoperators_pa_kernel(
     }
 
     with ExitStack() as ctx:
-        ctx.enter_context(tc.manual_schedule())
         const = ctx.enter_context(tc.tile_pool(name="const", bufs=1))
         keep = ctx.enter_context(tc.tile_pool(name="keep", bufs=1))
         w_raw_pool = ctx.enter_context(tc.tile_pool(name="w_raw", bufs=6))

@@ -10,7 +10,6 @@ U8 = mybir.dt.uint8
 I32 = mybir.dt.int32
 FP8X4 = mybir.dt.float8_e4m3fn_x4
 ADD = mybir.AluOpType.add
-SUBTRACT = mybir.AluOpType.subtract
 MULT = mybir.AluOpType.mult
 MAX = mybir.AluOpType.max
 RELU = mybir.ActivationFunctionType.Relu
@@ -26,11 +25,13 @@ NF = 1024
 PASSES = NF // K_PASS
 F_TILES = NF // P
 HALVES = NF // BANK
-TILES_PER_HALF = BANK // P
+QUARTERS = 4
+QW = NF // QUARTERS
+TILES_PER_QUARTER = QW // P
 CHUNK_RECEIVERS = BANK // NODES
 CHUNKS = GRAPHS * NODES // CHUNK_RECEIVERS
 ROW_TILES = BANK // P
-VECTOR_TILES = 3
+SCALAR_TILES = (1, 4, 6)
 SUM_LAG = 2
 
 FLOPS = 2 * (GRAPHS * NODES * NODES + 4 * GRAPHS * NODES) * NF * NF
@@ -55,13 +56,14 @@ def tile_compositionalkoopmanoperators_pa_kernel(
         const = ctx.enter_context(tc.tile_pool(name="const", bufs=1))
         keep = ctx.enter_context(tc.tile_pool(name="keep", bufs=1))
         w_raw_pool = ctx.enter_context(tc.tile_pool(name="w_raw", bufs=6))
-        w_grouped_pool = ctx.enter_context(tc.tile_pool(name="w_grouped", bufs=3))
+        late_raw_pool = ctx.enter_context(tc.tile_pool(name="late_raw", bufs=3))
+        w_grouped_pool = ctx.enter_context(tc.tile_pool(name="w_grouped", bufs=4))
         x_raw_pool = ctx.enter_context(tc.tile_pool(name="x_raw", bufs=3))
-        x_pool = ctx.enter_context(tc.tile_pool(name="x", bufs=2))
+        x_pool = ctx.enter_context(tc.tile_pool(name="x", bufs=3))
         send_pool = ctx.enter_context(tc.tile_pool(name="send", bufs=2))
         clip_pool = ctx.enter_context(tc.tile_pool(name="clip", bufs=4))
         junk_pool = ctx.enter_context(tc.tile_pool(name="junk", bufs=2))
-        result_pool = ctx.enter_context(tc.tile_pool(name="result", bufs=2))
+        result_pool = ctx.enter_context(tc.tile_pool(name="result", bufs=4))
         psum_t = ctx.enter_context(tc.psum_pool(name="psum_t", bufs=4))
         psum_e = ctx.enter_context(tc.psum_pool(name="psum_e", bufs=4))
 
@@ -75,15 +77,52 @@ def tile_compositionalkoopmanoperators_pa_kernel(
                 [P, PASSES, NF], U8, name="%s_scales" % weight, align_bytes=64
             )
 
-        ident = const.tile([P, P], F32)
-        make_identity(nc, ident[:])
-        ident_bf = const.tile([P, P], BF16)
-        nc.vector.tensor_copy(out=ident_bf[:], in_=ident[:])
+        w_raw = {}
+        x_raw = {}
 
-        def quantise_weight_piece(weight, g, h, regroup):
+        def load_early(weight, quarter):
+            cols = slice(QW * quarter, QW * (quarter + 1))
+            raw = w_raw_pool.tile([P, PASSES, 2, 2, QW], BF16)
+            rows = weight_rows[weight][:, cols].rearrange("(w p e) c -> p w e c", p=P, e=2)
+            raw_rows = raw[:].rearrange("p g u e c -> p (g u) e c")
+            for e in range(2):
+                nc.sync.dma_start(out=raw_rows[:, :, e, :], in_=rows[:, :, e, :])
+            w_raw[(weight, quarter)] = raw
+
+        def load_chunk(c):
+            raw = x_raw_pool.tile([P, ROW_TILES, NF], BF16)
+            rows = relations[BANK * c : BANK * (c + 1), :].rearrange("(r p) k -> p r k", p=P)
+            for pair in range(ROW_TILES // 2):
+                pair_rows = slice(2 * pair, 2 * pair + 2)
+                nc.sync.dma_start(out=raw[:, pair_rows, :], in_=rows[:, pair_rows, :])
+            x_raw[c] = raw
+
+        def regroup_and_quantise(weight, g, cols, raw, regroup):
+            grouped = w_grouped_pool.tile([P, BANK, PACK], BF16, align_bytes=64)
+            width = cols.stop - cols.start
+            regroup(
+                out=grouped[:, 0:width, :].rearrange("p (c i) t -> p c t i", i=4),
+                in_=raw.rearrange("p t (c i) -> p c t i", i=4),
+            )
+            nc.vector.quantize_mx(
+                out=w_codes[weight][:, g, cols].bitcast(FP8X4),
+                scales=w_scales[weight][:, g, cols],
+                in_=grouped[:, 0:width, :].rearrange("p c t -> p (c t)"),
+            )
+
+        def prepare_early(weight, quarter):
+            cols = slice(QW * quarter, QW * (quarter + 1))
+            raw = w_raw[(weight, quarter)]
+            for g in range(PASSES):
+                regroup = nc.vector.tensor_copy if g == 0 else nc.scalar.copy
+                regroup_and_quantise(
+                    weight, g, cols, raw[:, g].rearrange("p u e c -> p (u e) c"), regroup
+                )
+
+        def prepare_late(weight, h, g):
             cols = slice(BANK * h, BANK * (h + 1))
             rows = weight_rows[weight][K_PASS * g : K_PASS * (g + 1), cols]
-            raw = w_raw_pool.tile([P, PACK, BANK], BF16)
+            raw = late_raw_pool.tile([P, PACK, BANK], BF16)
             if weight == "pa":
                 nc.sync.dma_start(out=raw[:], in_=rows.rearrange("(t p) c -> p t c", p=P))
             else:
@@ -94,22 +133,27 @@ def tile_compositionalkoopmanoperators_pa_kernel(
                             "(p e) c -> p e c", e=2
                         ),
                     )
-            grouped = w_grouped_pool.tile([P, BANK, PACK], BF16, align_bytes=64)
-            regroup(
-                out=grouped[:].rearrange("p (c i) t -> p c t i", i=4),
-                in_=raw[:].rearrange("p t (c i) -> p c t i", i=4),
-            )
-            nc.vector.quantize_mx(
-                out=w_codes[weight][:, g, cols].bitcast(FP8X4),
-                scales=w_scales[weight][:, g, cols],
-                in_=grouped[:].rearrange("p c t -> p (c t)"),
-            )
+            regroup_and_quantise(weight, g, cols, raw[:], nc.vector.tensor_copy)
 
-        def early_weight(weight, h):
-            for g in range(PASSES):
-                quantise_weight_piece(
-                    weight, g, h, nc.vector.tensor_copy if g == 0 else nc.scalar.copy
-                )
+        first = const.tile([P, 1], F32)
+        nc.vector.memset(first[:], 0.0)
+        nc.scalar.activation(out=first[:], in_=first[:], func=RELU)
+
+        load_early("wr", 0)
+        load_chunk(0)
+        load_early("wj", 0)
+        obj_raw = const.tile([P, NF], BF16)
+        nc.sync.dma_start(out=obj_raw[:], in_=particles)
+        bias_rows = const.tile([P, P], BF16)
+        nc.vector.memset(bias_rows[:], 0.0)
+        nc.sync.dma_start(out=bias_rows[0:F_TILES, :], in_=rp_b.rearrange("(m p) -> m p", p=P))
+        load_early("wi", 0)
+        load_chunk(1)
+
+        ident = const.tile([P, P], F32)
+        make_identity(nc, ident[:])
+        ident_bf = const.tile([P, P], BF16)
+        nc.vector.tensor_copy(out=ident_bf[:], in_=ident[:])
 
         x_grouped = {}
         x_codes = {}
@@ -118,11 +162,6 @@ def tile_compositionalkoopmanoperators_pa_kernel(
         send_scales = {}
 
         def transpose_chunk(c):
-            x_raw = x_raw_pool.tile([P, ROW_TILES, NF], BF16)
-            nc.sync.dma_start(
-                out=x_raw[:],
-                in_=relations[BANK * c : BANK * (c + 1), :].rearrange("(r p) k -> p r k", p=P),
-            )
             grouped = x_pool.tile([P, PASSES, PACK * BANK], BF16, name="x_grouped", align_bytes=64)
             banks = {}
             for g in range(PASSES):
@@ -130,7 +169,7 @@ def tile_compositionalkoopmanoperators_pa_kernel(
                     xt = psum_t.tile([P, 2, 2 * P], F32, tag="small")
                     for u in range(2):
                         for r in range(2):
-                            words_in = x_raw[:, 2 * pair + r, :].bitcast(F32)
+                            words_in = x_raw[c][:, 2 * pair + r, :].bitcast(F32)
                             nc.tensor.transpose(
                                 xt[:, u, P * r : P * (r + 1)],
                                 words_in[:, P * (2 * g + u) : P * (2 * g + u + 1)],
@@ -181,13 +220,9 @@ def tile_compositionalkoopmanoperators_pa_kernel(
             if c * CHUNK_RECEIVERS % NODES == 0:
                 repeat_senders(c * CHUNK_RECEIVERS // NODES)
 
+        prepare_early("wr", 0)
         transpose_chunk(0)
-
-        obj_raw = const.tile([P, NF], BF16)
-        nc.sync.dma_start(out=obj_raw[:], in_=particles)
-        bias_rows = const.tile([P, P], BF16)
-        nc.vector.memset(bias_rows[:], 0.0)
-        nc.sync.dma_start(out=bias_rows[0:F_TILES, :], in_=rp_b.rearrange("(m p) -> m p", p=P))
+        prepare_early("wj", 0)
 
         obj_t = psum_t.tile([P, 2 * PASSES, P], F32, tag="small")
         for w in range(2 * PASSES):
@@ -207,7 +242,6 @@ def tile_compositionalkoopmanoperators_pa_kernel(
             scales=obj_scales[:].rearrange("p g r -> p (g r)"),
             in_=obj_grouped[:],
         )
-        quantise_chunk(0)
 
         bias_t = psum_t.tile([P, P], BF16, tag="small")
         nc.tensor.transpose(bias_t[:], bias_rows[:], ident_bf[:])
@@ -216,16 +250,17 @@ def tile_compositionalkoopmanoperators_pa_kernel(
         neg_rp_bias = const.tile([P, F_TILES], F32)
         nc.vector.tensor_scalar_mul(out=neg_rp_bias[:], in0=bias_t[:, 0:F_TILES], scalar1=-1.0)
 
-        neg_recv = keep.tile([P, PASSES, P, VECTOR_TILES], F32)
-        clipped_sum = keep.tile([P, PASSES, P, VECTOR_TILES], F32)
-        scalar_recv = keep.tile([P, PASSES, P], F32)
-        scalar_agg = keep.tile([P, PASSES, P], F32)
+        neg_recv = keep.tile([P, F_TILES, P], F32)
+        scalar_recv = keep.tile([P, F_TILES, P], F32)
+        sums = keep.tile([P, F_TILES, P], F32)
+        for f in SCALAR_TILES:
+            nc.gpsimd.memset(neg_recv[:, f, :], 0.0)
 
-        def receiver_terms(h):
-            first_tile = TILES_PER_HALF * h
-            bank = psum_t.tile([P, TILES_PER_HALF, P], F32, tag="small")
-            for q in range(TILES_PER_HALF):
-                f_cols = slice(BANK * h + P * q, BANK * h + P * (q + 1))
+        def receiver_terms(quarter):
+            bank = psum_t.tile([P, TILES_PER_QUARTER, P], F32, tag="small")
+            for q in range(TILES_PER_QUARTER):
+                f = TILES_PER_QUARTER * quarter + q
+                f_cols = slice(P * f, P * (f + 1))
                 for g in range(PASSES):
                     nc.tensor.matmul_mx(
                         out=bank[:, q, :],
@@ -236,28 +271,32 @@ def tile_compositionalkoopmanoperators_pa_kernel(
                         start=(g == 0),
                         stop=(g == PASSES - 1),
                     )
-            nc.vector.tensor_tensor(
-                out=neg_recv[:, h, :, :],
-                in0=neg_rp_bias[:, first_tile : first_tile + VECTOR_TILES]
-                .unsqueeze(1)
-                .to_broadcast([P, P, VECTOR_TILES]),
-                in1=bank[:, 0:VECTOR_TILES, :].rearrange("p q r -> p r q"),
-                op=SUBTRACT,
-            )
-            nc.scalar.activation(
-                out=scalar_recv[:, h, :],
-                in_=bank[:, VECTOR_TILES, :],
-                func=IDENTITY,
-                bias=rp_bias[:, first_tile + VECTOR_TILES : first_tile + VECTOR_TILES + 1],
-            )
+            for q in range(TILES_PER_QUARTER):
+                f = TILES_PER_QUARTER * quarter + q
+                if f in SCALAR_TILES:
+                    nc.scalar.activation(
+                        out=scalar_recv[:, f, :],
+                        in_=bank[:, q, :],
+                        func=IDENTITY,
+                        bias=rp_bias[:, f : f + 1],
+                    )
+                else:
+                    nc.vector.tensor_scalar(
+                        out=neg_recv[:, f, :],
+                        in0=bank[:, q, :],
+                        scalar1=-1.0,
+                        scalar2=neg_rp_bias[:, f : f + 1],
+                        op0=MULT,
+                        op1=ADD,
+                    )
 
-        def multiply_bank(c, h, q):
+        def multiply_bank(c, f):
             graph = c * CHUNK_RECEIVERS // NODES
             operands = (
                 ("wr", x_codes[c], x_scales[c]),
                 ("wj", send_codes[graph], send_scales[graph]),
             )
-            f_cols = slice(BANK * h + P * q, BANK * h + P * (q + 1))
+            f_cols = slice(P * f, P * (f + 1))
             acc = psum_e.tile([P, BANK], F32)
             for n, (weight, codes, scales) in enumerate(operands):
                 for g in range(PASSES):
@@ -272,17 +311,20 @@ def tile_compositionalkoopmanoperators_pa_kernel(
                     )
             return acc[:].rearrange("p (i j) -> p i j", j=NODES)
 
-        def clip_and_fold(x, c, h, q):
+        def clip(x, c, f):
             receivers = slice(c * CHUNK_RECEIVERS, (c + 1) * CHUNK_RECEIVERS)
             clipped = clip_pool.tile([P, CHUNK_RECEIVERS, NODES], F32)
             nc.vector.tensor_tensor(
                 out=clipped[:],
                 in0=x,
-                in1=neg_recv[:, h, receivers, q]
+                in1=neg_recv[:, f, receivers]
                 .unsqueeze(2)
                 .to_broadcast([P, CHUNK_RECEIVERS, NODES]),
                 op=MAX,
             )
+            return clipped, sums[:, f, receivers]
+
+        def fold(clipped):
             folded = clip_pool.tile([P, CHUNK_RECEIVERS, NODES // 2], F32)
             nc.gpsimd.tensor_tensor(
                 out=folded[:],
@@ -290,12 +332,12 @@ def tile_compositionalkoopmanoperators_pa_kernel(
                 in1=clipped[:, :, NODES // 2 : NODES],
                 op=ADD,
             )
-            return folded, clipped_sum[:, h, receivers, q]
+            return folded
 
         def sum_bank(folded, target):
             nc.vector.tensor_reduce(out=target, in_=folded[:], axis=mybir.AxisListType.X, op=ADD)
 
-        def scalar_sums(x, c, h):
+        def scalar_sums(x, c, f):
             junk = junk_pool.tile([P, CHUNK_RECEIVERS, NODES], F32)
             for i in range(CHUNK_RECEIVERS):
                 r = c * CHUNK_RECEIVERS + i
@@ -303,83 +345,142 @@ def tile_compositionalkoopmanoperators_pa_kernel(
                     out=junk[:, i, :],
                     in_=x[:, i, :],
                     func=RELU,
-                    bias=scalar_recv[:, h, r : r + 1],
-                    accum_out=scalar_agg[:, h, r : r + 1],
+                    bias=scalar_recv[:, f, r : r + 1],
+                    accum_out=sums[:, f, r : r + 1],
                 )
 
-        def early_half(h):
-            early_weight("wi", h)
-            receiver_terms(h)
-            early_weight("wr", h)
-            early_weight("wj", h)
+        waiting = []
 
-        early_half(0)
+        def unit(c, quarter):
+            for q in range(TILES_PER_QUARTER):
+                f = TILES_PER_QUARTER * quarter + q
+                x = multiply_bank(c, f)
+                if f in SCALAR_TILES:
+                    scalar_sums(x, c, f)
+                    continue
+                clipped, target = clip(x, c, f)
+                if c == CHUNKS - 1 and quarter == QUARTERS - 1:
+                    sum_bank(clipped, target)
+                    continue
+                waiting.append((fold(clipped), target))
+                if len(waiting) > SUM_LAG:
+                    sum_bank(*waiting.pop(0))
+
+        def flush():
+            while len(waiting) > 0:
+                sum_bank(*waiting.pop(0))
+
+        agg_bf = const.tile([P, PASSES, P, PACK], BF16, align_bytes=64)
+        agg_codes = const.tile([P, PASSES, P], U32, align_bytes=64)
+        agg_scales = const.tile([P, PASSES, P], U8, align_bytes=64)
+
+        def aggregate(g):
+            tiles = slice(PACK * g, PACK * (g + 1))
+            nc.vector.scalar_tensor_tensor(
+                out=agg_bf[:, g],
+                in0=neg_recv[:, tiles, :].rearrange("p t r -> p r t"),
+                scalar=-float(NODES),
+                in1=sums[:, tiles, :].rearrange("p t r -> p r t"),
+                op0=MULT,
+                op1=ADD,
+            )
+            nc.vector.quantize_mx(
+                out=agg_codes[:, g, :].bitcast(FP8X4),
+                scales=agg_scales[:, g, :],
+                in_=agg_bf[:, g].rearrange("p r t -> p (r t)"),
+            )
+
+        def prepare_quarter(quarter):
+            prepare_early("wi", quarter)
+            receiver_terms(quarter)
+            prepare_early("wr", quarter)
+            prepare_early("wj", quarter)
+
+        def load_quarter(quarter):
+            for weight in ("wi", "wr", "wj"):
+                load_early(weight, quarter)
+
+        quantise_chunk(0)
+        prepare_early("wi", 0)
+        receiver_terms(0)
         transpose_chunk(1)
+        load_quarter(1)
+        unit(0, 0)
+        quantise_chunk(1)
+        prepare_quarter(1)
+        load_quarter(2)
+        unit(1, 0)
+        unit(0, 1)
+        prepare_quarter(2)
+        load_quarter(3)
+        load_chunk(2)
+        unit(1, 1)
+        unit(0, 2)
+        prepare_quarter(3)
+        load_chunk(3)
+        transpose_chunk(2)
+        unit(1, 2)
+        unit(0, 3)
+        quantise_chunk(2)
+        transpose_chunk(3)
+        unit(1, 3)
 
-        late_pieces = [
-            (weight, g, h) for weight in ("po", "pa") for h in range(HALVES) for g in range(PASSES)
-        ]
-        folded_banks = []
-        for c in range(CHUNKS):
-            for h in range(HALVES):
-                for q in range(TILES_PER_HALF):
-                    x = multiply_bank(c, h, q)
-                    if q < VECTOR_TILES:
-                        folded_banks.append(clip_and_fold(x, c, h, q))
-                        if len(folded_banks) > SUM_LAG:
-                            sum_bank(*folded_banks[len(folded_banks) - 1 - SUM_LAG])
-                    else:
-                        scalar_sums(x, c, h)
-                if h == 0:
-                    if c == 0:
-                        early_half(1)
+        late = [(w, h, g) for w in ("po", "pa") for h in range(HALVES) for g in range(PASSES)]
+        for c in range(2, CHUNKS):
+            for quarter in range(QUARTERS):
+                unit(c, quarter)
+                if quarter == 1:
                     if c + 1 < CHUNKS:
                         quantise_chunk(c + 1)
                     if c + 2 < CHUNKS:
+                        load_chunk(c + 2)
                         transpose_chunk(c + 2)
-                    quantise_weight_piece(*late_pieces[c], nc.vector.tensor_copy)
-        for n in range(len(folded_banks) - SUM_LAG, len(folded_banks)):
-            sum_bank(*folded_banks[n])
+                if quarter % 2 == 0 and len(late) > 0:
+                    prepare_late(*late.pop(0))
+                if c == CHUNKS - 1 and quarter == 2:
+                    flush()
+                    aggregate(0)
 
         pp_bias = const.tile([P, NF], BF16)
         nc.sync.dma_start(out=pp_bias[:], in_=pp_b.partition_broadcast(P))
 
-        agg_bf = const.tile([P, PASSES * P * PACK], BF16, align_bytes=64)
-        agg_words = agg_bf[:].rearrange("p (w t) -> p w t", t=PACK)
-        nc.vector.scalar_tensor_tensor(
-            out=agg_words[:, :, 0:VECTOR_TILES],
-            in0=neg_recv[:].rearrange("p g r t -> p (g r) t"),
-            scalar=-float(NODES),
-            in1=clipped_sum[:].rearrange("p g r t -> p (g r) t"),
-            op0=MULT,
-            op1=ADD,
-        )
-        nc.vector.tensor_copy(
-            out=agg_words[:, :, VECTOR_TILES], in_=scalar_agg[:].rearrange("p g r -> p (g r)")
-        )
-        agg_codes = const.tile([P, PASSES, P], U32, align_bytes=64)
-        agg_scales = const.tile([P, PASSES, P], U8, align_bytes=64)
-        nc.vector.quantize_mx(
-            out=agg_codes[:].rearrange("p g r -> p (g r)").bitcast(FP8X4),
-            scales=agg_scales[:].rearrange("p g r -> p (g r)"),
-            in_=agg_bf[:],
-        )
+        totals = []
         for h in range(HALVES):
-            cols = slice(BANK * h, BANK * (h + 1))
             total = psum_e.tile([P, BANK], F32, tag="acc")
-            products = (("po", obj_codes, obj_scales), ("pa", agg_codes, agg_scales))
-            for n, (weight, codes, scales) in enumerate(products):
-                for g in range(PASSES):
-                    nc.tensor.matmul_mx(
-                        out=total[:],
-                        lhsT=codes[:, g, :].bitcast(FP8X4),
-                        lhsT_scale=scales[:, g, :],
-                        rhs=w_codes[weight][:, g, cols].bitcast(FP8X4),
-                        rhs_scale=w_scales[weight][:, g, cols],
-                        start=(n == 0 and g == 0),
-                        stop=(n == 1 and g == PASSES - 1),
-                    )
-            result = result_pool.tile([P, BANK], F32)
-            nc.vector.tensor_tensor(out=result[:], in0=total[:], in1=pp_bias[:, cols], op=ADD)
-            nc.scalar.activation(out=result[:], in_=result[:], func=RELU)
-            nc.sync.dma_start(out=out_rows[:, cols], in_=result[:])
+            totals.append(total)
+        products = (
+            ("po", obj_codes, obj_scales, 0),
+            ("po", obj_codes, obj_scales, 1),
+            ("pa", agg_codes, agg_scales, 0),
+            ("pa", agg_codes, agg_scales, 1),
+        )
+
+        def last_product(h, n):
+            weight, codes, scales, g = products[n]
+            cols = slice(BANK * h, BANK * (h + 1))
+            nc.tensor.matmul_mx(
+                out=totals[h][:],
+                lhsT=codes[:, g, :].bitcast(FP8X4),
+                lhsT_scale=scales[:, g, :],
+                rhs=w_codes[weight][:, g, cols].bitcast(FP8X4),
+                rhs_scale=w_scales[weight][:, g, cols],
+                start=(n == 0),
+                stop=(n == len(products) - 1),
+            )
+
+        for h in range(HALVES):
+            for n in range(len(products) - 1):
+                last_product(h, n)
+        aggregate(1)
+        for h in range(HALVES):
+            last_product(h, len(products) - 1)
+        for h in range(HALVES):
+            for part in range(2):
+                here = slice(QW * part, QW * (part + 1))
+                cols = slice(BANK * h + QW * part, BANK * h + QW * (part + 1))
+                result = result_pool.tile([P, QW], F32)
+                nc.vector.tensor_tensor(
+                    out=result[:], in0=totals[h][:, here], in1=pp_bias[:, cols], op=ADD
+                )
+                nc.scalar.activation(out=result[:], in_=result[:], func=RELU)
+                nc.sync.dma_start(out=out_rows[:, cols], in_=result[:])

@@ -32,6 +32,7 @@ CHUNK_RECEIVERS = BANK // NODES
 CHUNKS = GRAPHS * NODES // CHUNK_RECEIVERS
 ROW_TILES = BANK // P
 SCALAR_TILES = (1, 4, 6)
+OPEN = 6
 SUM_LAG = 2
 
 FLOPS = 2 * (GRAPHS * NODES * NODES + 4 * GRAPHS * NODES) * NF * NF
@@ -56,16 +57,16 @@ def tile_compositionalkoopmanoperators_pa_kernel(
         const = ctx.enter_context(tc.tile_pool(name="const", bufs=1))
         keep = ctx.enter_context(tc.tile_pool(name="keep", bufs=1))
         w_raw_pool = ctx.enter_context(tc.tile_pool(name="w_raw", bufs=6))
-        late_raw_pool = ctx.enter_context(tc.tile_pool(name="late_raw", bufs=3))
-        w_grouped_pool = ctx.enter_context(tc.tile_pool(name="w_grouped", bufs=4))
+        w_grouped_pool = ctx.enter_context(tc.tile_pool(name="w_grouped", bufs=8))
         x_raw_pool = ctx.enter_context(tc.tile_pool(name="x_raw", bufs=3))
-        x_pool = ctx.enter_context(tc.tile_pool(name="x", bufs=3))
+        x_pool = ctx.enter_context(tc.tile_pool(name="x", bufs=2))
         send_pool = ctx.enter_context(tc.tile_pool(name="send", bufs=2))
         clip_pool = ctx.enter_context(tc.tile_pool(name="clip", bufs=4))
         junk_pool = ctx.enter_context(tc.tile_pool(name="junk", bufs=2))
         result_pool = ctx.enter_context(tc.tile_pool(name="result", bufs=4))
-        psum_t = ctx.enter_context(tc.psum_pool(name="psum_t", bufs=4))
-        psum_e = ctx.enter_context(tc.psum_pool(name="psum_e", bufs=4))
+        psum_t = ctx.enter_context(tc.psum_pool(name="psum_t", bufs=2))
+        psum_e = ctx.enter_context(tc.psum_pool(name="psum_e", bufs=6))
+        ctx.enter_context(tc.manual_schedule())
 
         w_codes = {}
         w_scales = {}
@@ -80,14 +81,17 @@ def tile_compositionalkoopmanoperators_pa_kernel(
         w_raw = {}
         x_raw = {}
 
-        def load_early(weight, quarter):
-            cols = slice(QW * quarter, QW * (quarter + 1))
-            raw = w_raw_pool.tile([P, PASSES, 2, 2, QW], BF16)
-            rows = weight_rows[weight][:, cols].rearrange("(w p e) c -> p w e c", p=P, e=2)
-            raw_rows = raw[:].rearrange("p g u e c -> p (g u) e c")
-            for e in range(2):
-                nc.sync.dma_start(out=raw_rows[:, :, e, :], in_=rows[:, :, e, :])
-            w_raw[(weight, quarter)] = raw
+        def load_weight(weight, g):
+            rows = weight_rows[weight][K_PASS * g : K_PASS * (g + 1), :]
+            raw = w_raw_pool.tile([P, PACK, NF], BF16)
+            if weight == "pa":
+                nc.sync.dma_start(out=raw[:], in_=rows.rearrange("(t p) c -> p t c", p=P))
+            else:
+                nc.sync.dma_start(
+                    out=raw[:].rearrange("p (u e) c -> p u (e c)", e=2),
+                    in_=rows.rearrange("(u p e) c -> p u (e c)", p=P, e=2),
+                )
+            w_raw[(weight, g)] = raw
 
         def load_chunk(c):
             raw = x_raw_pool.tile([P, ROW_TILES, NF], BF16)
@@ -97,59 +101,56 @@ def tile_compositionalkoopmanoperators_pa_kernel(
                 nc.sync.dma_start(out=raw[:, pair_rows, :], in_=rows[:, pair_rows, :])
             x_raw[c] = raw
 
-        def regroup_and_quantise(weight, g, cols, raw, regroup):
-            grouped = w_grouped_pool.tile([P, BANK, PACK], BF16, align_bytes=64)
-            width = cols.stop - cols.start
-            regroup(
-                out=grouped[:, 0:width, :].rearrange("p (c i) t -> p c t i", i=4),
-                in_=raw.rearrange("p t (c i) -> p c t i", i=4),
-            )
+        w_grouped = {}
+
+        def regroup(weight, quarter, g, by):
+            raw = w_raw[(weight, g)][:, :, QW * quarter : QW * (quarter + 1)]
+            grouped = w_grouped_pool.tile([P, QW, PACK], BF16, align_bytes=64)
+            if by == "tensor":
+                bank = psum_t.tile([P, QW, PACK], BF16, tag="small")
+                for half in range(2):
+                    cols = slice(P * half, P * (half + 1))
+                    nc.tensor.matmul(
+                        out=bank[:, cols, :].rearrange("p c t -> p (c t)"),
+                        lhsT=ident_bf[:],
+                        rhs=raw[:, :, cols].rearrange("p t c -> p c t"),
+                        start=True,
+                        stop=True,
+                    )
+                nc.scalar.copy(out=grouped[:], in_=bank[:])
+            else:
+                copy = nc.vector.tensor_copy if by == "vector" else nc.scalar.copy
+                copy(
+                    out=grouped[:].rearrange("p (c i) t -> p c t i", i=4),
+                    in_=raw.rearrange("p t (c i) -> p c t i", i=4),
+                )
+            w_grouped[(weight, quarter, g)] = grouped
+
+        def quantise(weight, quarter, g):
+            cols = slice(QW * quarter, QW * (quarter + 1))
             nc.vector.quantize_mx(
                 out=w_codes[weight][:, g, cols].bitcast(FP8X4),
                 scales=w_scales[weight][:, g, cols],
-                in_=grouped[:, 0:width, :].rearrange("p c t -> p (c t)"),
+                in_=w_grouped[(weight, quarter, g)][:].rearrange("p c t -> p (c t)"),
             )
-
-        def prepare_early(weight, quarter):
-            cols = slice(QW * quarter, QW * (quarter + 1))
-            raw = w_raw[(weight, quarter)]
-            for g in range(PASSES):
-                regroup = nc.vector.tensor_copy if g == 0 else nc.scalar.copy
-                regroup_and_quantise(
-                    weight, g, cols, raw[:, g].rearrange("p u e c -> p (u e) c"), regroup
-                )
-
-        def prepare_late(weight, h, g):
-            cols = slice(BANK * h, BANK * (h + 1))
-            rows = weight_rows[weight][K_PASS * g : K_PASS * (g + 1), cols]
-            raw = late_raw_pool.tile([P, PACK, BANK], BF16)
-            if weight == "pa":
-                nc.sync.dma_start(out=raw[:], in_=rows.rearrange("(t p) c -> p t c", p=P))
-            else:
-                for u in range(2):
-                    nc.sync.dma_start(
-                        out=raw[:, 2 * u : 2 * u + 2, :],
-                        in_=rows[2 * P * u : 2 * P * (u + 1), :].rearrange(
-                            "(p e) c -> p e c", e=2
-                        ),
-                    )
-            regroup_and_quantise(weight, g, cols, raw[:], nc.vector.tensor_copy)
 
         first = const.tile([P, 1], F32)
         nc.vector.memset(first[:], 0.0)
         nc.scalar.activation(out=first[:], in_=first[:], func=RELU)
 
-        load_early("wr", 0)
+        load_weight("wr", 0)
         load_chunk(0)
-        load_early("wj", 0)
+        load_weight("wr", 1)
         obj_raw = const.tile([P, NF], BF16)
         nc.sync.dma_start(out=obj_raw[:], in_=particles)
         bias_rows = const.tile([P, P], BF16)
         nc.vector.memset(bias_rows[:], 0.0)
         nc.sync.dma_start(out=bias_rows[0:F_TILES, :], in_=rp_b.rearrange("(m p) -> m p", p=P))
-        load_early("wi", 0)
+        load_weight("wj", 0)
+        load_weight("wj", 1)
+        load_weight("wi", 0)
+        load_weight("wi", 1)
         load_chunk(1)
-
         ident = const.tile([P, P], F32)
         make_identity(nc, ident[:])
         ident_bf = const.tile([P, P], BF16)
@@ -161,29 +162,34 @@ def tile_compositionalkoopmanoperators_pa_kernel(
         send_codes = {}
         send_scales = {}
 
-        def transpose_chunk(c):
-            grouped = x_pool.tile([P, PASSES, PACK * BANK], BF16, name="x_grouped", align_bytes=64)
-            banks = {}
-            for g in range(PASSES):
-                for pair in range(ROW_TILES // 2):
-                    xt = psum_t.tile([P, 2, 2 * P], F32, tag="small")
-                    for u in range(2):
-                        for r in range(2):
-                            words_in = x_raw[c][:, 2 * pair + r, :].bitcast(F32)
-                            nc.tensor.transpose(
-                                xt[:, u, P * r : P * (r + 1)],
-                                words_in[:, P * (2 * g + u) : P * (2 * g + u + 1)],
-                                ident[:],
-                            )
-                    banks[(g, pair)] = xt
-            for g in range(PASSES):
-                words_out = grouped[:, g, :].bitcast(F32).rearrange("p (c u) -> p c u", u=2)
-                for pair in range(ROW_TILES // 2):
-                    nc.scalar.copy(
-                        out=words_out[:, 2 * P * pair : 2 * P * (pair + 1), :],
-                        in_=banks[(g, pair)][:].rearrange("p u c -> p c u"),
-                    )
-            x_grouped[c] = grouped
+        x_banks = {}
+
+        def transpose_banks(c, first, last):
+            for b in range(first, last):
+                g, pair = b // 2, b % 2
+                xt = psum_t.tile([P, 2, 2 * P], F32, tag="small")
+                for u in range(2):
+                    for r in range(2):
+                        words_in = x_raw[c][:, 2 * pair + r, :].bitcast(F32)
+                        nc.tensor.transpose(
+                            xt[:, u, P * r : P * (r + 1)],
+                            words_in[:, P * (2 * g + u) : P * (2 * g + u + 1)],
+                            ident[:],
+                        )
+                x_banks[(c, b)] = xt
+
+        def copy_banks(c, first, last):
+            if first == 0:
+                x_grouped[c] = x_pool.tile(
+                    [P, PASSES, PACK * BANK], BF16, name="x_grouped", align_bytes=64
+                )
+            for b in range(first, last):
+                g, pair = b // 2, b % 2
+                words_out = x_grouped[c][:, g, :].bitcast(F32).rearrange("p (c u) -> p c u", u=2)
+                nc.scalar.copy(
+                    out=words_out[:, 2 * P * pair : 2 * P * (pair + 1), :],
+                    in_=x_banks[(c, b)][:].rearrange("p u c -> p c u"),
+                )
 
         def repeat_senders(graph):
             senders = slice(NODES * graph, NODES * (graph + 1))
@@ -206,49 +212,45 @@ def tile_compositionalkoopmanoperators_pa_kernel(
             send_codes[graph] = rep_codes
             send_scales[graph] = rep_scales
 
-        def quantise_chunk(c):
-            codes = x_pool.tile([P, PASSES, BANK], U32, name="x_codes", align_bytes=64)
-            scales = x_pool.tile([P, PASSES, BANK], U8, name="x_scales", align_bytes=64)
-            for g in range(PASSES):
-                nc.vector.quantize_mx(
-                    out=codes[:, g, :].bitcast(FP8X4),
-                    scales=scales[:, g, :],
-                    in_=x_grouped[c][:, g, :],
-                )
-            x_codes[c] = codes
-            x_scales[c] = scales
-            if c * CHUNK_RECEIVERS % NODES == 0:
-                repeat_senders(c * CHUNK_RECEIVERS // NODES)
-
-        prepare_early("wr", 0)
-        transpose_chunk(0)
-        prepare_early("wj", 0)
-
-        obj_t = psum_t.tile([P, 2 * PASSES, P], F32, tag="small")
-        for w in range(2 * PASSES):
-            nc.tensor.transpose(
-                obj_t[:, w, :], obj_raw[:].bitcast(F32)[:, P * w : P * (w + 1)], ident[:]
+        def quantise_chunk(c, g):
+            if g == 0:
+                x_codes[c] = x_pool.tile([P, PASSES, BANK], U32, name="x_codes", align_bytes=64)
+                x_scales[c] = x_pool.tile([P, PASSES, BANK], U8, name="x_scales", align_bytes=64)
+            nc.vector.quantize_mx(
+                out=x_codes[c][:, g, :].bitcast(FP8X4),
+                scales=x_scales[c][:, g, :],
+                in_=x_grouped[c][:, g, :],
             )
-        obj_grouped = const.tile([P, PASSES * P * PACK], BF16, align_bytes=64)
-        nc.scalar.copy(
-            out=obj_grouped[:].bitcast(F32).rearrange("p (g r u) -> p g r u", g=PASSES, u=2),
-            in_=obj_t[:].rearrange("p (g u) r -> p g r u", u=2),
-        )
+
         obj_codes = const.tile([P, PASSES, P], U32, align_bytes=64)
         obj_scales = const.tile([P, PASSES, P], U8, align_bytes=64)
         nc.vector.memset(obj_scales[:].bitcast(I32), 0)
-        nc.vector.quantize_mx(
-            out=obj_codes[:].rearrange("p g r -> p (g r)").bitcast(FP8X4),
-            scales=obj_scales[:].rearrange("p g r -> p (g r)"),
-            in_=obj_grouped[:],
-        )
 
-        bias_t = psum_t.tile([P, P], BF16, tag="small")
-        nc.tensor.transpose(bias_t[:], bias_rows[:], ident_bf[:])
+        def prepare_particles():
+            obj_t = psum_t.tile([P, 2 * PASSES, P], F32, tag="small")
+            for w in range(2 * PASSES):
+                nc.tensor.transpose(
+                    obj_t[:, w, :], obj_raw[:].bitcast(F32)[:, P * w : P * (w + 1)], ident[:]
+                )
+            obj_grouped = const.tile([P, PASSES * P * PACK], BF16, align_bytes=64)
+            nc.scalar.copy(
+                out=obj_grouped[:].bitcast(F32).rearrange("p (g r u) -> p g r u", g=PASSES, u=2),
+                in_=obj_t[:].rearrange("p (g u) r -> p g r u", u=2),
+            )
+            nc.vector.quantize_mx(
+                out=obj_codes[:].rearrange("p g r -> p (g r)").bitcast(FP8X4),
+                scales=obj_scales[:].rearrange("p g r -> p (g r)"),
+                in_=obj_grouped[:],
+            )
+
         rp_bias = const.tile([P, F_TILES], F32)
-        nc.vector.tensor_copy(out=rp_bias[:], in_=bias_t[:, 0:F_TILES])
         neg_rp_bias = const.tile([P, F_TILES], F32)
-        nc.vector.tensor_scalar_mul(out=neg_rp_bias[:], in0=bias_t[:, 0:F_TILES], scalar1=-1.0)
+
+        def prepare_bias():
+            bias_t = psum_t.tile([P, P], BF16, tag="small")
+            nc.tensor.transpose(bias_t[:], bias_rows[:], ident_bf[:])
+            nc.vector.tensor_copy(out=rp_bias[:], in_=bias_t[:, 0:F_TILES])
+            nc.vector.tensor_scalar_mul(out=neg_rp_bias[:], in0=bias_t[:, 0:F_TILES], scalar1=-1.0)
 
         neg_recv = keep.tile([P, F_TILES, P], F32)
         scalar_recv = keep.tile([P, F_TILES, P], F32)
@@ -256,7 +258,9 @@ def tile_compositionalkoopmanoperators_pa_kernel(
         for f in SCALAR_TILES:
             nc.gpsimd.memset(neg_recv[:, f, :], 0.0)
 
-        def receiver_terms(quarter):
+        recv_banks = {}
+
+        def multiply_receivers(quarter):
             bank = psum_t.tile([P, TILES_PER_QUARTER, P], F32, tag="small")
             for q in range(TILES_PER_QUARTER):
                 f = TILES_PER_QUARTER * quarter + q
@@ -271,6 +275,10 @@ def tile_compositionalkoopmanoperators_pa_kernel(
                         start=(g == 0),
                         stop=(g == PASSES - 1),
                     )
+            recv_banks[quarter] = bank
+
+        def receiver_terms(quarter):
+            bank = recv_banks[quarter]
             for q in range(TILES_PER_QUARTER):
                 f = TILES_PER_QUARTER * quarter + q
                 if f in SCALAR_TILES:
@@ -290,26 +298,33 @@ def tile_compositionalkoopmanoperators_pa_kernel(
                         op1=ADD,
                     )
 
-        def multiply_bank(c, f):
-            graph = c * CHUNK_RECEIVERS // NODES
-            operands = (
-                ("wr", x_codes[c], x_scales[c]),
-                ("wj", send_codes[graph], send_scales[graph]),
-            )
+        x_acc = {}
+
+        def multiply_part(c, f, weight, g):
+            if weight == "wr":
+                codes, scales = x_codes[c], x_scales[c]
+            else:
+                graph = c * CHUNK_RECEIVERS // NODES
+                codes, scales = send_codes[graph], send_scales[graph]
             f_cols = slice(P * f, P * (f + 1))
-            acc = psum_e.tile([P, BANK], F32)
-            for n, (weight, codes, scales) in enumerate(operands):
+            first = weight == "wr" and g == 0
+            if first:
+                acc = psum_e.tile([P, BANK], F32)
+                x_acc[(c, f)] = acc
+            nc.tensor.matmul_mx(
+                out=x_acc[(c, f)][:],
+                lhsT=w_codes[weight][:, g, f_cols].bitcast(FP8X4),
+                lhsT_scale=w_scales[weight][:, g, f_cols],
+                rhs=codes[:, g, :].bitcast(FP8X4),
+                rhs_scale=scales[:, g, :],
+                start=first,
+                stop=(weight == "wj" and g == PASSES - 1),
+            )
+
+        def multiply_bank(c, f):
+            for weight in ("wr", "wj"):
                 for g in range(PASSES):
-                    nc.tensor.matmul_mx(
-                        out=acc[:],
-                        lhsT=w_codes[weight][:, g, f_cols].bitcast(FP8X4),
-                        lhsT_scale=w_scales[weight][:, g, f_cols],
-                        rhs=codes[:, g, :].bitcast(FP8X4),
-                        rhs_scale=scales[:, g, :],
-                        start=(n == 0 and g == 0),
-                        stop=(n == 1 and g == PASSES - 1),
-                    )
-            return acc[:].rearrange("p (i j) -> p i j", j=NODES)
+                    multiply_part(c, f, weight, g)
 
         def clip(x, c, f):
             receivers = slice(c * CHUNK_RECEIVERS, (c + 1) * CHUNK_RECEIVERS)
@@ -351,23 +366,16 @@ def tile_compositionalkoopmanoperators_pa_kernel(
 
         waiting = []
 
-        def unit(c, quarter):
-            for q in range(TILES_PER_QUARTER):
-                f = TILES_PER_QUARTER * quarter + q
-                x = multiply_bank(c, f)
-                if f in SCALAR_TILES:
-                    scalar_sums(x, c, f)
-                    continue
-                clipped, target = clip(x, c, f)
-                if c == CHUNKS - 1 and quarter == QUARTERS - 1:
-                    sum_bank(clipped, target)
-                    continue
-                waiting.append((fold(clipped), target))
-                if len(waiting) > SUM_LAG:
-                    sum_bank(*waiting.pop(0))
+        def drain_bank(c, f, folded=True):
+            x = x_acc[(c, f)][:].rearrange("p (i j) -> p i j", j=NODES)
+            if f in SCALAR_TILES:
+                scalar_sums(x, c, f)
+                return
+            clipped, target = clip(x, c, f)
+            waiting.append((fold(clipped) if folded else clipped, target))
 
-        def flush():
-            while len(waiting) > 0:
+        def sum_waiting(keep_back):
+            while len(waiting) > keep_back:
                 sum_bank(*waiting.pop(0))
 
         agg_bf = const.tile([P, PASSES, P, PACK], BF16, align_bytes=64)
@@ -390,57 +398,92 @@ def tile_compositionalkoopmanoperators_pa_kernel(
                 in_=agg_bf[:, g].rearrange("p r t -> p (r t)"),
             )
 
-        def prepare_quarter(quarter):
-            prepare_early("wi", quarter)
-            receiver_terms(quarter)
-            prepare_early("wr", quarter)
-            prepare_early("wj", quarter)
 
-        def load_quarter(quarter):
-            for weight in ("wi", "wr", "wj"):
-                load_early(weight, quarter)
+        def transpose_chunk(c, half):
+            transpose_banks(c, 2 * half, 2 * half + 2)
+            copy_banks(c, 2 * half, 2 * half + 2)
 
-        quantise_chunk(0)
-        prepare_early("wi", 0)
-        receiver_terms(0)
-        transpose_chunk(1)
-        load_quarter(1)
-        unit(0, 0)
-        quantise_chunk(1)
-        prepare_quarter(1)
-        load_quarter(2)
-        unit(1, 0)
-        unit(0, 1)
-        prepare_quarter(2)
-        load_quarter(3)
-        load_chunk(2)
-        unit(1, 1)
-        unit(0, 2)
-        prepare_quarter(3)
-        load_chunk(3)
-        transpose_chunk(2)
-        unit(1, 2)
-        unit(0, 3)
-        quantise_chunk(2)
-        transpose_chunk(3)
-        unit(1, 3)
-
-        late = [(w, h, g) for w in ("po", "pa") for h in range(HALVES) for g in range(PASSES)]
-        for c in range(2, CHUNKS):
+        def prepare_pass(weight, g, by_vector):
             for quarter in range(QUARTERS):
-                unit(c, quarter)
-                if quarter == 1:
-                    if c + 1 < CHUNKS:
-                        quantise_chunk(c + 1)
-                    if c + 2 < CHUNKS:
-                        load_chunk(c + 2)
-                        transpose_chunk(c + 2)
-                if quarter % 2 == 0 and len(late) > 0:
-                    prepare_late(*late.pop(0))
-                if c == CHUNKS - 1 and quarter == 2:
-                    flush()
-                    aggregate(0)
+                regroup(weight, quarter, g, "vector" if quarter < by_vector else "tensor")
 
+        def quantise_pass(weight, g):
+            for quarter in range(QUARTERS):
+                quantise(weight, quarter, g)
+
+        prepare_pass("wr", 0, 2)
+        transpose_chunk(0, 0)
+        transpose_chunk(0, 1)
+        quantise_pass("wr", 0)
+        prepare_pass("wr", 1, 2)
+        quantise_chunk(0, 0)
+        quantise_chunk(0, 1)
+        for f in range(OPEN):
+            multiply_part(0, f, "wr", 0)
+        quantise_pass("wr", 1)
+        prepare_particles()
+        prepare_pass("wj", 0, 1)
+        repeat_senders(0)
+        for f in range(OPEN):
+            multiply_part(0, f, "wr", 1)
+        quantise_pass("wj", 0)
+        prepare_pass("wj", 1, 2)
+        for f in range(OPEN):
+            multiply_part(0, f, "wj", 0)
+        quantise_pass("wj", 1)
+        prepare_bias()
+        prepare_pass("wi", 0, 1)
+        for f in range(OPEN):
+            multiply_part(0, f, "wj", 1)
+        quantise_pass("wi", 0)
+        prepare_pass("wi", 1, 2)
+        transpose_chunk(1, 0)
+        quantise_pass("wi", 1)
+        transpose_chunk(1, 1)
+        for quarter in range(QUARTERS):
+            multiply_receivers(quarter)
+            receiver_terms(quarter)
+        quantise_chunk(1, 0)
+        quantise_chunk(1, 1)
+
+        late = [(weight, g) for weight in ("po", "pa") for g in range(PASSES)]
+        late_pieces = [(weight, quarter, g) for weight, g in late for quarter in range(QUARTERS)]
+        slot = 0
+        for c in range(CHUNKS):
+            for f in range(F_TILES):
+                if c > 0 or f >= OPEN:
+                    multiply_bank(c, f)
+                last = c == CHUNKS - 1 and f >= F_TILES - 2
+                drain_bank(c, f, folded=not last)
+                if slot == 0:
+                    load_chunk(2)
+                if slot % 12 == 8 and slot // 12 < len(late):
+                    load_weight(*late[slot // 12])
+                n = slot - 14
+                if n >= 0 and n // 3 < len(late_pieces):
+                    if n % 3 == 0:
+                        regroup(*late_pieces[n // 3], "vector")
+                    if n % 3 == 1:
+                        quantise(*late_pieces[n // 3])
+                if 0 < c < CHUNKS - 1:
+                    if f == 3:
+                        quantise_chunk(c + 1, 0)
+                    if f == 5:
+                        quantise_chunk(c + 1, 1)
+                if c < CHUNKS - 1:
+                    if f == 6 and (c + 1) * CHUNK_RECEIVERS % NODES == 0:
+                        repeat_senders((c + 1) * CHUNK_RECEIVERS // NODES)
+                if c + 2 < CHUNKS:
+                    if f == 0 and c > 0:
+                        load_chunk(c + 2)
+                    if f == 4:
+                        transpose_chunk(c + 2, 0)
+                    if f == 6:
+                        transpose_chunk(c + 2, 1)
+                sum_waiting(0 if last else SUM_LAG)
+                slot += 1
+                if c == CHUNKS - 1 and f == F_TILES - 2:
+                    aggregate(0)
         pp_bias = const.tile([P, NF], BF16)
         nc.sync.dma_start(out=pp_bias[:], in_=pp_b.partition_broadcast(P))
 

@@ -106,24 +106,11 @@ def tile_compositionalkoopmanoperators_pa_kernel(
         def regroup(weight, quarter, g, by):
             raw = w_raw[(weight, g)][:, :, QW * quarter : QW * (quarter + 1)]
             grouped = w_grouped_pool.tile([P, QW, PACK], BF16, align_bytes=64)
-            if by == "tensor":
-                bank = psum_t.tile([P, QW, PACK], BF16, tag="small")
-                for half in range(2):
-                    cols = slice(P * half, P * (half + 1))
-                    nc.tensor.matmul(
-                        out=bank[:, cols, :].rearrange("p c t -> p (c t)"),
-                        lhsT=ident_bf[:],
-                        rhs=raw[:, :, cols].rearrange("p t c -> p c t"),
-                        start=True,
-                        stop=True,
-                    )
-                nc.scalar.copy(out=grouped[:], in_=bank[:])
-            else:
-                copy = nc.vector.tensor_copy if by == "vector" else nc.scalar.copy
-                copy(
-                    out=grouped[:].rearrange("p (c i) t -> p c t i", i=4),
-                    in_=raw.rearrange("p t (c i) -> p c t i", i=4),
-                )
+            copy = nc.vector.tensor_copy if by == "vector" else nc.scalar.copy
+            copy(
+                out=grouped[:].rearrange("p (c i) t -> p c t i", i=4),
+                in_=raw.rearrange("p t (c i) -> p c t i", i=4),
+            )
             w_grouped[(weight, quarter, g)] = grouped
 
         def quantise(weight, quarter, g):
@@ -405,38 +392,38 @@ def tile_compositionalkoopmanoperators_pa_kernel(
 
         def prepare_pass(weight, g, by_vector):
             for quarter in range(QUARTERS):
-                regroup(weight, quarter, g, "vector" if quarter < by_vector else "tensor")
+                regroup(weight, quarter, g, "vector" if quarter < by_vector else "scalar")
 
         def quantise_pass(weight, g):
             for quarter in range(QUARTERS):
                 quantise(weight, quarter, g)
 
-        prepare_pass("wr", 0, 2)
+        prepare_pass("wr", 0, 3)
         transpose_chunk(0, 0)
         transpose_chunk(0, 1)
         quantise_pass("wr", 0)
-        prepare_pass("wr", 1, 2)
+        prepare_pass("wr", 1, 3)
         quantise_chunk(0, 0)
         quantise_chunk(0, 1)
         for f in range(OPEN):
             multiply_part(0, f, "wr", 0)
         quantise_pass("wr", 1)
         prepare_particles()
-        prepare_pass("wj", 0, 1)
+        prepare_pass("wj", 0, 2)
         repeat_senders(0)
         for f in range(OPEN):
             multiply_part(0, f, "wr", 1)
         quantise_pass("wj", 0)
-        prepare_pass("wj", 1, 2)
+        prepare_pass("wj", 1, 3)
         for f in range(OPEN):
             multiply_part(0, f, "wj", 0)
         quantise_pass("wj", 1)
         prepare_bias()
-        prepare_pass("wi", 0, 1)
+        prepare_pass("wi", 0, 2)
         for f in range(OPEN):
             multiply_part(0, f, "wj", 1)
         quantise_pass("wi", 0)
-        prepare_pass("wi", 1, 2)
+        prepare_pass("wi", 1, 3)
         transpose_chunk(1, 0)
         quantise_pass("wi", 1)
         transpose_chunk(1, 1)
@@ -466,9 +453,9 @@ def tile_compositionalkoopmanoperators_pa_kernel(
                     if n % 3 == 1:
                         quantise(*late_pieces[n // 3])
                 if 0 < c < CHUNKS - 1:
-                    if f == 3:
+                    if f == 4:
                         quantise_chunk(c + 1, 0)
-                    if f == 5:
+                    if f == 6:
                         quantise_chunk(c + 1, 1)
                 if c < CHUNKS - 1:
                     if f == 6 and (c + 1) * CHUNK_RECEIVERS % NODES == 0:
@@ -476,10 +463,12 @@ def tile_compositionalkoopmanoperators_pa_kernel(
                 if c + 2 < CHUNKS:
                     if f == 0 and c > 0:
                         load_chunk(c + 2)
-                    if f == 4:
+                    if f == (7 if c == 0 else 4):
                         transpose_chunk(c + 2, 0)
-                    if f == 6:
+                    if f == 6 and c > 0:
                         transpose_chunk(c + 2, 1)
+                if c == 1 and f == 1:
+                    transpose_chunk(2, 1)
                 sum_waiting(0 if last else SUM_LAG)
                 slot += 1
                 if c == CHUNKS - 1 and f == F_TILES - 2:

@@ -32,7 +32,8 @@ CHUNK_RECEIVERS = BANK // NODES
 CHUNKS = GRAPHS * NODES // CHUNK_RECEIVERS
 ROW_TILES = BANK // P
 SCALAR_TILES = (1, 4, 6)
-OPEN = 6
+OUTER_TILES = (2, 5)
+OPEN = 5
 SUM_LAG = 2
 
 FLOPS = 2 * (GRAPHS * NODES * NODES + 4 * GRAPHS * NODES) * NF * NF
@@ -62,10 +63,12 @@ def tile_compositionalkoopmanoperators_pa_kernel(
         x_pool = ctx.enter_context(tc.tile_pool(name="x", bufs=2))
         send_pool = ctx.enter_context(tc.tile_pool(name="send", bufs=2))
         clip_pool = ctx.enter_context(tc.tile_pool(name="clip", bufs=4))
+        threshold_pool = ctx.enter_context(tc.tile_pool(name="threshold", bufs=3))
+        mean_pool = ctx.enter_context(tc.tile_pool(name="mean", bufs=2))
         junk_pool = ctx.enter_context(tc.tile_pool(name="junk", bufs=2))
         result_pool = ctx.enter_context(tc.tile_pool(name="result", bufs=4))
-        psum_t = ctx.enter_context(tc.psum_pool(name="psum_t", bufs=2))
-        psum_e = ctx.enter_context(tc.psum_pool(name="psum_e", bufs=6))
+        psum_t = ctx.enter_context(tc.psum_pool(name="psum_t", bufs=3))
+        psum_e = ctx.enter_context(tc.psum_pool(name="psum_e", bufs=5))
         ctx.enter_context(tc.manual_schedule())
 
         w_codes = {}
@@ -244,6 +247,11 @@ def tile_compositionalkoopmanoperators_pa_kernel(
         sums = keep.tile([P, F_TILES, P], F32)
         for f in SCALAR_TILES:
             nc.gpsimd.memset(neg_recv[:, f, :], 0.0)
+        outer_recv = {}
+        send = {}
+        for f in OUTER_TILES:
+            outer_recv[f] = keep.tile([P, P], F32, name="outer_recv_%d" % f)
+            send[f] = keep.tile([P, P], F32, name="send_%d" % f)
 
         recv_banks = {}
 
@@ -277,13 +285,59 @@ def tile_compositionalkoopmanoperators_pa_kernel(
                     )
                 else:
                     nc.vector.tensor_scalar(
-                        out=neg_recv[:, f, :],
+                        out=outer_recv[f][:] if f in OUTER_TILES else neg_recv[:, f, :],
                         in0=bank[:, q, :],
                         scalar1=-1.0,
                         scalar2=neg_rp_bias[:, f : f + 1],
                         op0=MULT,
                         op1=ADD,
                     )
+
+        def sender_terms(f):
+            f_cols = slice(P * f, P * (f + 1))
+            bank = psum_t.tile([P, P], F32, tag="small")
+            for g in range(PASSES):
+                nc.tensor.matmul_mx(
+                    out=bank[:],
+                    lhsT=w_codes["wj"][:, g, f_cols].bitcast(FP8X4),
+                    lhsT_scale=w_scales["wj"][:, g, f_cols],
+                    rhs=obj_codes[:, g, :].bitcast(FP8X4),
+                    rhs_scale=obj_scales[:, g, :],
+                    start=(g == 0),
+                    stop=(g == PASSES - 1),
+                )
+            nc.scalar.copy(out=send[f][:], in_=bank[:])
+
+        def outer_means(f):
+            by_graph = send[f][:].rearrange("p (b j) -> p b j", j=NODES)
+            total = mean_pool.tile([P, GRAPHS], F32)
+            nc.vector.tensor_reduce(
+                out=total[:], in_=by_graph, axis=mybir.AxisListType.X, op=ADD
+            )
+            nc.vector.scalar_tensor_tensor(
+                out=neg_recv[:, f, :].rearrange("p (b i) -> p b i", i=NODES),
+                in0=total[:].unsqueeze(2).to_broadcast([P, GRAPHS, NODES]),
+                scalar=-1.0 / NODES,
+                in1=outer_recv[f][:].rearrange("p (b i) -> p b i", i=NODES),
+                op0=MULT,
+                op1=ADD,
+            )
+
+        thresholds = {}
+
+        def make_threshold(c, f):
+            graph = c * CHUNK_RECEIVERS // NODES
+            threshold = threshold_pool.tile([P, CHUNK_RECEIVERS, NODES], F32)
+            for i in range(CHUNK_RECEIVERS):
+                r = c * CHUNK_RECEIVERS + i
+                nc.scalar.activation(
+                    out=threshold[:, i, :],
+                    in_=send[f][:, NODES * graph : NODES * (graph + 1)],
+                    func=IDENTITY,
+                    scale=-1.0,
+                    bias=outer_recv[f][:, r : r + 1],
+                )
+            thresholds[(c, f)] = threshold
 
         x_acc = {}
 
@@ -295,6 +349,7 @@ def tile_compositionalkoopmanoperators_pa_kernel(
                 codes, scales = send_codes[graph], send_scales[graph]
             f_cols = slice(P * f, P * (f + 1))
             first = weight == "wr" and g == 0
+            last = "wr" if f in OUTER_TILES else "wj"
             if first:
                 acc = psum_e.tile([P, BANK], F32)
                 x_acc[(c, f)] = acc
@@ -305,11 +360,11 @@ def tile_compositionalkoopmanoperators_pa_kernel(
                 rhs=codes[:, g, :].bitcast(FP8X4),
                 rhs_scale=scales[:, g, :],
                 start=first,
-                stop=(weight == "wj" and g == PASSES - 1),
+                stop=(weight == last and g == PASSES - 1),
             )
 
         def multiply_bank(c, f):
-            for weight in ("wr", "wj"):
+            for weight in ("wr",) if f in OUTER_TILES else ("wr", "wj"):
                 for g in range(PASSES):
                     multiply_part(c, f, weight, g)
 
@@ -319,7 +374,9 @@ def tile_compositionalkoopmanoperators_pa_kernel(
             nc.vector.tensor_tensor(
                 out=clipped[:],
                 in0=x,
-                in1=neg_recv[:, f, receivers]
+                in1=thresholds[(c, f)][:]
+                if f in OUTER_TILES
+                else neg_recv[:, f, receivers]
                 .unsqueeze(2)
                 .to_broadcast([P, CHUNK_RECEIVERS, NODES]),
                 op=MAX,
@@ -416,12 +473,16 @@ def tile_compositionalkoopmanoperators_pa_kernel(
         quantise_pass("wj", 0)
         prepare_pass("wj", 1, 3)
         for f in range(OPEN):
-            multiply_part(0, f, "wj", 0)
+            if f not in OUTER_TILES:
+                multiply_part(0, f, "wj", 0)
         quantise_pass("wj", 1)
         prepare_bias()
         prepare_pass("wi", 0, 2)
         for f in range(OPEN):
-            multiply_part(0, f, "wj", 1)
+            if f not in OUTER_TILES:
+                multiply_part(0, f, "wj", 1)
+        for f in OUTER_TILES:
+            sender_terms(f)
         quantise_pass("wi", 0)
         prepare_pass("wi", 1, 3)
         transpose_chunk(1, 0)
@@ -430,6 +491,8 @@ def tile_compositionalkoopmanoperators_pa_kernel(
         for quarter in range(QUARTERS):
             multiply_receivers(quarter)
             receiver_terms(quarter)
+        for f in OUTER_TILES:
+            make_threshold(0, f)
         quantise_chunk(1, 0)
         quantise_chunk(1, 1)
 
@@ -442,6 +505,10 @@ def tile_compositionalkoopmanoperators_pa_kernel(
                     multiply_bank(c, f)
                 last = c == CHUNKS - 1 and f >= F_TILES - 2
                 drain_bank(c, f, folded=not last)
+                if f in OUTER_TILES and c + 1 < CHUNKS:
+                    make_threshold(c + 1, f)
+                if c == 1 and f in OUTER_TILES:
+                    outer_means(f)
                 if slot == 0:
                     load_chunk(2)
                 if slot % 12 == 8 and slot // 12 < len(late):

@@ -34,6 +34,7 @@ ROW_TILES = BANK // P
 SCALAR_TILES = (1, 4, 6)
 OUTER_TILES = (2, 5)
 OPEN = 5
+EARLY_TILE, EARLY_CHUNKS = 1, 3
 SUM_LAG = 2
 
 FLOPS = 2 * (GRAPHS * NODES * NODES + 4 * GRAPHS * NODES) * NF * NF
@@ -130,12 +131,12 @@ def tile_compositionalkoopmanoperators_pa_kernel(
 
         load_weight("wr", 0)
         load_chunk(0)
-        load_weight("wr", 1)
         obj_raw = const.tile([P, NF], BF16)
         nc.sync.dma_start(out=obj_raw[:], in_=particles)
         bias_rows = const.tile([P, P], BF16)
         nc.vector.memset(bias_rows[:], 0.0)
         nc.sync.dma_start(out=bias_rows[0:F_TILES, :], in_=rp_b.rearrange("(m p) -> m p", p=P))
+        load_weight("wr", 1)
         load_weight("wj", 0)
         load_weight("wj", 1)
         load_weight("wi", 0)
@@ -246,7 +247,8 @@ def tile_compositionalkoopmanoperators_pa_kernel(
         scalar_recv = keep.tile([P, F_TILES, P], F32)
         sums = keep.tile([P, F_TILES, P], F32)
         for f in SCALAR_TILES:
-            nc.gpsimd.memset(neg_recv[:, f, :], 0.0)
+            count = EARLY_CHUNKS * CHUNK_RECEIVERS if f == EARLY_TILE else 0
+            nc.gpsimd.memset(neg_recv[:, f, count:P], 0.0)
         outer_recv = {}
         send = {}
         for f in OUTER_TILES:
@@ -276,6 +278,7 @@ def tile_compositionalkoopmanoperators_pa_kernel(
             bank = recv_banks[quarter]
             for q in range(TILES_PER_QUARTER):
                 f = TILES_PER_QUARTER * quarter + q
+                count = EARLY_CHUNKS * CHUNK_RECEIVERS if f == EARLY_TILE else P
                 if f in SCALAR_TILES:
                     nc.scalar.activation(
                         out=scalar_recv[:, f, :],
@@ -283,10 +286,11 @@ def tile_compositionalkoopmanoperators_pa_kernel(
                         func=IDENTITY,
                         bias=rp_bias[:, f : f + 1],
                     )
-                else:
+                if f not in SCALAR_TILES or f == EARLY_TILE:
+                    target = outer_recv[f] if f in OUTER_TILES else neg_recv[:, f, :]
                     nc.vector.tensor_scalar(
-                        out=outer_recv[f][:] if f in OUTER_TILES else neg_recv[:, f, :],
-                        in0=bank[:, q, :],
+                        out=target[:, 0:count],
+                        in0=bank[:, q, 0:count],
                         scalar1=-1.0,
                         scalar2=neg_rp_bias[:, f : f + 1],
                         op0=MULT,
@@ -412,7 +416,7 @@ def tile_compositionalkoopmanoperators_pa_kernel(
 
         def drain_bank(c, f, folded=True):
             x = x_acc[(c, f)][:].rearrange("p (i j) -> p i j", j=NODES)
-            if f in SCALAR_TILES:
+            if f in SCALAR_TILES and not (f == EARLY_TILE and c < EARLY_CHUNKS):
                 scalar_sums(x, c, f)
                 return
             clipped, target = clip(x, c, f)
@@ -460,23 +464,23 @@ def tile_compositionalkoopmanoperators_pa_kernel(
         transpose_chunk(0, 1)
         quantise_pass("wr", 0)
         prepare_pass("wr", 1, 3)
+        prepare_particles()
         quantise_chunk(0, 0)
         quantise_chunk(0, 1)
+        prepare_bias()
         for f in range(OPEN):
             multiply_part(0, f, "wr", 0)
         quantise_pass("wr", 1)
-        prepare_particles()
         prepare_pass("wj", 0, 2)
         repeat_senders(0)
         for f in range(OPEN):
             multiply_part(0, f, "wr", 1)
         quantise_pass("wj", 0)
-        prepare_pass("wj", 1, 3)
+        prepare_pass("wj", 1, 2)
         for f in range(OPEN):
             if f not in OUTER_TILES:
                 multiply_part(0, f, "wj", 0)
         quantise_pass("wj", 1)
-        prepare_bias()
         prepare_pass("wi", 0, 2)
         for f in range(OPEN):
             if f not in OUTER_TILES:
@@ -484,7 +488,7 @@ def tile_compositionalkoopmanoperators_pa_kernel(
         for f in OUTER_TILES:
             sender_terms(f)
         quantise_pass("wi", 0)
-        prepare_pass("wi", 1, 3)
+        prepare_pass("wi", 1, 2)
         transpose_chunk(1, 0)
         quantise_pass("wi", 1)
         transpose_chunk(1, 1)
@@ -520,9 +524,9 @@ def tile_compositionalkoopmanoperators_pa_kernel(
                     if n % 3 == 1:
                         quantise(*late_pieces[n // 3])
                 if 0 < c < CHUNKS - 1:
-                    if f == 4:
+                    if f == 1:
                         quantise_chunk(c + 1, 0)
-                    if f == 6:
+                    if f == 3:
                         quantise_chunk(c + 1, 1)
                 if c < CHUNKS - 1:
                     if f == 6 and (c + 1) * CHUNK_RECEIVERS % NODES == 0:
@@ -530,9 +534,9 @@ def tile_compositionalkoopmanoperators_pa_kernel(
                 if c + 2 < CHUNKS:
                     if f == 0 and c > 0:
                         load_chunk(c + 2)
-                    if f == (7 if c == 0 else 4):
+                    if f == (7 if c == 0 else 5):
                         transpose_chunk(c + 2, 0)
-                    if f == 6 and c > 0:
+                    if f == 7 and c > 0:
                         transpose_chunk(c + 2, 1)
                 if c == 1 and f == 1:
                     transpose_chunk(2, 1)

@@ -131,17 +131,18 @@ def tile_compositionalkoopmanoperators_pa_kernel(
 
         load_weight("wr", 0)
         load_chunk(0)
+        load_weight("wr", 1)
         obj_raw = const.tile([P, NF], BF16)
         nc.sync.dma_start(out=obj_raw[:], in_=particles)
         bias_rows = const.tile([P, P], BF16)
         nc.vector.memset(bias_rows[:], 0.0)
         nc.sync.dma_start(out=bias_rows[0:F_TILES, :], in_=rp_b.rearrange("(m p) -> m p", p=P))
-        load_weight("wr", 1)
         load_weight("wj", 0)
         load_weight("wj", 1)
         load_weight("wi", 0)
         load_weight("wi", 1)
         load_chunk(1)
+
         ident = const.tile([P, P], F32)
         make_identity(nc, ident[:])
         ident_bf = const.tile([P, P], BF16)
@@ -420,7 +421,7 @@ def tile_compositionalkoopmanoperators_pa_kernel(
                 scalar_sums(x, c, f)
                 return
             clipped, target = clip(x, c, f)
-            waiting.append((fold(clipped) if folded else clipped, target))
+            waiting.append((fold(clipped) if folded and f != 3 else clipped, target))
 
         def sum_waiting(keep_back):
             while len(waiting) > keep_back:
@@ -507,7 +508,7 @@ def tile_compositionalkoopmanoperators_pa_kernel(
             for f in range(F_TILES):
                 if c > 0 or f >= OPEN:
                     multiply_bank(c, f)
-                last = c == CHUNKS - 1 and f >= F_TILES - 2
+                last = c == CHUNKS - 1 and f == F_TILES - 1
                 drain_bank(c, f, folded=not last)
                 if f in OUTER_TILES and c + 1 < CHUNKS:
                     make_threshold(c + 1, f)
@@ -540,10 +541,11 @@ def tile_compositionalkoopmanoperators_pa_kernel(
                         transpose_chunk(c + 2, 1)
                 if c == 1 and f == 1:
                     transpose_chunk(2, 1)
+                if c == CHUNKS - 1 and f == F_TILES - 3:
+                    sum_waiting(1)
+                    aggregate(0)
                 sum_waiting(0 if last else SUM_LAG)
                 slot += 1
-                if c == CHUNKS - 1 and f == F_TILES - 2:
-                    aggregate(0)
         pp_bias = const.tile([P, NF], BF16)
         nc.sync.dma_start(out=pp_bias[:], in_=pp_b.partition_broadcast(P))
 

@@ -112,8 +112,8 @@ def tile_compositionalkoopmanoperators_pa_kernel(
             grouped = w_grouped_pool.tile([P, QW, PACK], BF16, align_bytes=64)
             copy = nc.vector.tensor_copy if by == "vector" else nc.scalar.copy
             copy(
-                out=grouped[:].rearrange("p (c i) t -> p c t i", i=4),
-                in_=raw.rearrange("p t (c i) -> p c t i", i=4),
+                out=grouped[:].rearrange("p (c i) t -> p c t i", i=8),
+                in_=raw.rearrange("p t (c i) -> p c t i", i=8),
             )
             w_grouped[(weight, quarter, g)] = grouped
 

from contextlib import ExitStack

import concourse.mybir as mybir
from concourse.masks import make_identity

F32 = mybir.dt.float32
BF16 = mybir.dt.bfloat16
U32 = mybir.dt.uint32
U8 = mybir.dt.uint8
I32 = mybir.dt.int32
FP8X4 = mybir.dt.float8_e4m3fn_x4
ADD = mybir.AluOpType.add
MULT = mybir.AluOpType.mult
MAX = mybir.AluOpType.max
RELU = mybir.ActivationFunctionType.Relu
IDENTITY = mybir.ActivationFunctionType.Identity

P = 128
PACK = 4
K_PASS = P * PACK
BANK = 512
GRAPHS = 4
NODES = 32
NF = 1024
PASSES = NF // K_PASS
F_TILES = NF // P
HALVES = NF // BANK
QUARTERS = 4
QW = NF // QUARTERS
TILES_PER_QUARTER = QW // P
CHUNK_RECEIVERS = BANK // NODES
CHUNKS = GRAPHS * NODES // CHUNK_RECEIVERS
ROW_TILES = BANK // P
SCALAR_TILES = (1, 4, 6)
OUTER_TILES = (2, 5)
OPEN = 5
EARLY_TILE, EARLY_CHUNKS = 1, 3
SUM_LAG = 2

FLOPS = 2 * (GRAPHS * NODES * NODES + 4 * GRAPHS * NODES) * NF * NF


def tile_compositionalkoopmanoperators_pa_kernel(
    tc, rel_enc, obj, rp_w, rp_b, pp_w, pp_b, out
):
    nc = tc.nc
    relations = rel_enc.rearrange("b i j k -> (b i j) k")
    particles = obj.rearrange("b i k -> (b i) k")
    out_rows = out.rearrange("b i f -> (b i) f")
    weight_rows = {
        "wr": rp_w[0:NF, :],
        "wi": rp_w[NF : 2 * NF, :],
        "wj": rp_w[2 * NF : 3 * NF, :],
        "po": pp_w[0:NF, :],
        "pa": pp_w[NF : 2 * NF, :],
    }

    with ExitStack() as ctx:
        const = ctx.enter_context(tc.tile_pool(name="const", bufs=1))
        keep = ctx.enter_context(tc.tile_pool(name="keep", bufs=1))
        w_raw_pool = ctx.enter_context(tc.tile_pool(name="w_raw", bufs=6))
        w_grouped_pool = ctx.enter_context(tc.tile_pool(name="w_grouped", bufs=8))
        x_raw_pool = ctx.enter_context(tc.tile_pool(name="x_raw", bufs=3))
        x_pool = ctx.enter_context(tc.tile_pool(name="x", bufs=2))
        send_pool = ctx.enter_context(tc.tile_pool(name="send", bufs=2))
        clip_pool = ctx.enter_context(tc.tile_pool(name="clip", bufs=4))
        threshold_pool = ctx.enter_context(tc.tile_pool(name="threshold", bufs=3))
        mean_pool = ctx.enter_context(tc.tile_pool(name="mean", bufs=2))
        junk_pool = ctx.enter_context(tc.tile_pool(name="junk", bufs=2))
        result_pool = ctx.enter_context(tc.tile_pool(name="result", bufs=4))
        psum_t = ctx.enter_context(tc.psum_pool(name="psum_t", bufs=3))
        psum_e = ctx.enter_context(tc.psum_pool(name="psum_e", bufs=5))
        ctx.enter_context(tc.manual_schedule())

        w_codes = {}
        w_scales = {}
        for weight in weight_rows:
            w_codes[weight] = keep.tile(
                [P, PASSES, NF], U32, name="%s_codes" % weight, align_bytes=64
            )
            w_scales[weight] = keep.tile(
                [P, PASSES, NF], U8, name="%s_scales" % weight, align_bytes=64
            )

        w_raw = {}
        x_raw = {}

        def load_weight(weight, g):
            rows = weight_rows[weight][K_PASS * g : K_PASS * (g + 1), :]
            raw = w_raw_pool.tile([P, PACK, NF], BF16)
            if weight == "pa":
                nc.sync.dma_start(out=raw[:], in_=rows.rearrange("(t p) c -> p t c", p=P))
            else:
                nc.sync.dma_start(
                    out=raw[:].rearrange("p (u e) c -> p u (e c)", e=2),
                    in_=rows.rearrange("(u p e) c -> p u (e c)", p=P, e=2),
                )
            w_raw[(weight, g)] = raw

        def load_chunk(c):
            raw = x_raw_pool.tile([P, ROW_TILES, NF], BF16)
            rows = relations[BANK * c : BANK * (c + 1), :].rearrange("(r p) k -> p r k", p=P)
            for pair in range(ROW_TILES // 2):
                pair_rows = slice(2 * pair, 2 * pair + 2)
                nc.sync.dma_start(out=raw[:, pair_rows, :], in_=rows[:, pair_rows, :])
            x_raw[c] = raw

        w_grouped = {}

        def regroup(weight, quarter, g, by):
            raw = w_raw[(weight, g)][:, :, QW * quarter : QW * (quarter + 1)]
            grouped = w_grouped_pool.tile([P, QW, PACK], BF16, align_bytes=64)
            copy = nc.vector.tensor_copy if by == "vector" else nc.scalar.copy
            copy(
                out=grouped[:].rearrange("p (c i) t -> p c t i", i=8),
                in_=raw.rearrange("p t (c i) -> p c t i", i=8),
            )
            w_grouped[(weight, quarter, g)] = grouped

        def quantise(weight, quarter, g):
            cols = slice(QW * quarter, QW * (quarter + 1))
            nc.vector.quantize_mx(
                out=w_codes[weight][:, g, cols].bitcast(FP8X4),
                scales=w_scales[weight][:, g, cols],
                in_=w_grouped[(weight, quarter, g)][:].rearrange("p c t -> p (c t)"),
            )

        first = const.tile([P, 1], F32)
        nc.vector.memset(first[:], 0.0)
        nc.scalar.activation(out=first[:], in_=first[:], func=RELU)

        load_weight("wr", 0)
        load_chunk(0)
        load_weight("wr", 1)
        obj_raw = const.tile([P, NF], BF16)
        nc.sync.dma_start(out=obj_raw[:], in_=particles)
        bias_rows = const.tile([P, P], BF16)
        nc.vector.memset(bias_rows[:], 0.0)
        nc.sync.dma_start(out=bias_rows[0:F_TILES, :], in_=rp_b.rearrange("(m p) -> m p", p=P))
        load_weight("wj", 0)
        load_weight("wj", 1)
        load_weight("wi", 0)
        load_weight("wi", 1)
        load_chunk(1)

        ident = const.tile([P, P], F32)
        make_identity(nc, ident[:])
        ident_bf = const.tile([P, P], BF16)
        nc.vector.tensor_copy(out=ident_bf[:], in_=ident[:])

        x_grouped = {}
        x_codes = {}
        x_scales = {}
        send_codes = {}
        send_scales = {}

        x_banks = {}

        def transpose_banks(c, first, last):
            for b in range(first, last):
                g, pair = b // 2, b % 2
                xt = psum_t.tile([P, 2, 2 * P], F32, tag="small")
                for u in range(2):
                    for r in range(2):
                        words_in = x_raw[c][:, 2 * pair + r, :].bitcast(F32)
                        nc.tensor.transpose(
                            xt[:, u, P * r : P * (r + 1)],
                            words_in[:, P * (2 * g + u) : P * (2 * g + u + 1)],
                            ident[:],
                        )
                x_banks[(c, b)] = xt

        def copy_banks(c, first, last):
            if first == 0:
                x_grouped[c] = x_pool.tile(
                    [P, PASSES, PACK * BANK], BF16, name="x_grouped", align_bytes=64
                )
            for b in range(first, last):
                g, pair = b // 2, b % 2
                words_out = x_grouped[c][:, g, :].bitcast(F32).rearrange("p (c u) -> p c u", u=2)
                nc.scalar.copy(
                    out=words_out[:, 2 * P * pair : 2 * P * (pair + 1), :],
                    in_=x_banks[(c, b)][:].rearrange("p u c -> p c u"),
                )

        def repeat_senders(graph):
            senders = slice(NODES * graph, NODES * (graph + 1))
            rep_codes = send_pool.tile([P, PASSES, BANK], U32, align_bytes=64)
            rep_scales = send_pool.tile([P, PASSES, BANK], U8, align_bytes=64)
            nc.vector.tensor_copy(
                out=rep_codes[:].bitcast(I32).rearrange("p g (i j) -> p g i j", j=NODES),
                in_=obj_codes[:, :, senders]
                .bitcast(I32)
                .unsqueeze(2)
                .to_broadcast([P, PASSES, CHUNK_RECEIVERS, NODES]),
            )
            nc.vector.tensor_copy(
                out=rep_scales[:].bitcast(I32).rearrange("p g (i w) -> p g i w", w=NODES // 4),
                in_=obj_scales[:, :, senders]
                .bitcast(I32)
                .unsqueeze(2)
                .to_broadcast([P, PASSES, CHUNK_RECEIVERS, NODES // 4]),
            )
            send_codes[graph] = rep_codes
            send_scales[graph] = rep_scales

        def quantise_chunk(c, g):
            if g == 0:
                x_codes[c] = x_pool.tile([P, PASSES, BANK], U32, name="x_codes", align_bytes=64)
                x_scales[c] = x_pool.tile([P, PASSES, BANK], U8, name="x_scales", align_bytes=64)
            nc.vector.quantize_mx(
                out=x_codes[c][:, g, :].bitcast(FP8X4),
                scales=x_scales[c][:, g, :],
                in_=x_grouped[c][:, g, :],
            )

        obj_codes = const.tile([P, PASSES, P], U32, align_bytes=64)
        obj_scales = const.tile([P, PASSES, P], U8, align_bytes=64)
        nc.vector.memset(obj_scales[:].bitcast(I32), 0)

        def prepare_particles():
            obj_t = psum_t.tile([P, 2 * PASSES, P], F32, tag="small")
            for w in range(2 * PASSES):
                nc.tensor.transpose(
                    obj_t[:, w, :], obj_raw[:].bitcast(F32)[:, P * w : P * (w + 1)], ident[:]
                )
            obj_grouped = const.tile([P, PASSES * P * PACK], BF16, align_bytes=64)
            nc.scalar.copy(
                out=obj_grouped[:].bitcast(F32).rearrange("p (g r u) -> p g r u", g=PASSES, u=2),
                in_=obj_t[:].rearrange("p (g u) r -> p g r u", u=2),
            )
            nc.vector.quantize_mx(
                out=obj_codes[:].rearrange("p g r -> p (g r)").bitcast(FP8X4),
                scales=obj_scales[:].rearrange("p g r -> p (g r)"),
                in_=obj_grouped[:],
            )

        rp_bias = const.tile([P, F_TILES], F32)
        neg_rp_bias = const.tile([P, F_TILES], F32)

        def prepare_bias():
            bias_t = psum_t.tile([P, P], BF16, tag="small")
            nc.tensor.transpose(bias_t[:], bias_rows[:], ident_bf[:])
            nc.vector.tensor_copy(out=rp_bias[:], in_=bias_t[:, 0:F_TILES])
            nc.vector.tensor_scalar_mul(out=neg_rp_bias[:], in0=bias_t[:, 0:F_TILES], scalar1=-1.0)

        neg_recv = keep.tile([P, F_TILES, P], F32)
        scalar_recv = keep.tile([P, F_TILES, P], F32)
        sums = keep.tile([P, F_TILES, P], F32)
        for f in SCALAR_TILES:
            count = EARLY_CHUNKS * CHUNK_RECEIVERS if f == EARLY_TILE else 0
            nc.gpsimd.memset(neg_recv[:, f, count:P], 0.0)
        outer_recv = {}
        send = {}
        for f in OUTER_TILES:
            outer_recv[f] = keep.tile([P, P], F32, name="outer_recv_%d" % f)
            send[f] = keep.tile([P, P], F32, name="send_%d" % f)

        recv_banks = {}

        def multiply_receivers(quarter):
            bank = psum_t.tile([P, TILES_PER_QUARTER, P], F32, tag="small")
            for q in range(TILES_PER_QUARTER):
                f = TILES_PER_QUARTER * quarter + q
                f_cols = slice(P * f, P * (f + 1))
                for g in range(PASSES):
                    nc.tensor.matmul_mx(
                        out=bank[:, q, :],
                        lhsT=w_codes["wi"][:, g, f_cols].bitcast(FP8X4),
                        lhsT_scale=w_scales["wi"][:, g, f_cols],
                        rhs=obj_codes[:, g, :].bitcast(FP8X4),
                        rhs_scale=obj_scales[:, g, :],
                        start=(g == 0),
                        stop=(g == PASSES - 1),
                    )
            recv_banks[quarter] = bank

        def receiver_terms(quarter):
            bank = recv_banks[quarter]
            for q in range(TILES_PER_QUARTER):
                f = TILES_PER_QUARTER * quarter + q
                count = EARLY_CHUNKS * CHUNK_RECEIVERS if f == EARLY_TILE else P
                if f in SCALAR_TILES:
                    nc.scalar.activation(
                        out=scalar_recv[:, f, :],
                        in_=bank[:, q, :],
                        func=IDENTITY,
                        bias=rp_bias[:, f : f + 1],
                    )
                if f not in SCALAR_TILES or f == EARLY_TILE:
                    target = outer_recv[f] if f in OUTER_TILES else neg_recv[:, f, :]
                    nc.vector.tensor_scalar(
                        out=target[:, 0:count],
                        in0=bank[:, q, 0:count],
                        scalar1=-1.0,
                        scalar2=neg_rp_bias[:, f : f + 1],
                        op0=MULT,
                        op1=ADD,
                    )

        def sender_terms(f):
            f_cols = slice(P * f, P * (f + 1))
            bank = psum_t.tile([P, P], F32, tag="small")
            for g in range(PASSES):
                nc.tensor.matmul_mx(
                    out=bank[:],
                    lhsT=w_codes["wj"][:, g, f_cols].bitcast(FP8X4),
                    lhsT_scale=w_scales["wj"][:, g, f_cols],
                    rhs=obj_codes[:, g, :].bitcast(FP8X4),
                    rhs_scale=obj_scales[:, g, :],
                    start=(g == 0),
                    stop=(g == PASSES - 1),
                )
            nc.scalar.copy(out=send[f][:], in_=bank[:])

        def outer_means(f):
            by_graph = send[f][:].rearrange("p (b j) -> p b j", j=NODES)
            total = mean_pool.tile([P, GRAPHS], F32)
            nc.vector.tensor_reduce(
                out=total[:], in_=by_graph, axis=mybir.AxisListType.X, op=ADD
            )
            nc.vector.scalar_tensor_tensor(
                out=neg_recv[:, f, :].rearrange("p (b i) -> p b i", i=NODES),
                in0=total[:].unsqueeze(2).to_broadcast([P, GRAPHS, NODES]),
                scalar=-1.0 / NODES,
                in1=outer_recv[f][:].rearrange("p (b i) -> p b i", i=NODES),
                op0=MULT,
                op1=ADD,
            )

        thresholds = {}

        def make_threshold(c, f):
            graph = c * CHUNK_RECEIVERS // NODES
            threshold = threshold_pool.tile([P, CHUNK_RECEIVERS, NODES], F32)
            for i in range(CHUNK_RECEIVERS):
                r = c * CHUNK_RECEIVERS + i
                nc.scalar.activation(
                    out=threshold[:, i, :],
                    in_=send[f][:, NODES * graph : NODES * (graph + 1)],
                    func=IDENTITY,
                    scale=-1.0,
                    bias=outer_recv[f][:, r : r + 1],
                )
            thresholds[(c, f)] = threshold

        x_acc = {}

        def multiply_part(c, f, weight, g):
            if weight == "wr":
                codes, scales = x_codes[c], x_scales[c]
            else:
                graph = c * CHUNK_RECEIVERS // NODES
                codes, scales = send_codes[graph], send_scales[graph]
            f_cols = slice(P * f, P * (f + 1))
            first = weight == "wr" and g == 0
            last = "wr" if f in OUTER_TILES else "wj"
            if first:
                acc = psum_e.tile([P, BANK], F32)
                x_acc[(c, f)] = acc
            nc.tensor.matmul_mx(
                out=x_acc[(c, f)][:],
                lhsT=w_codes[weight][:, g, f_cols].bitcast(FP8X4),
                lhsT_scale=w_scales[weight][:, g, f_cols],
                rhs=codes[:, g, :].bitcast(FP8X4),
                rhs_scale=scales[:, g, :],
                start=first,
                stop=(weight == last and g == PASSES - 1),
            )

        def multiply_bank(c, f):
            for weight in ("wr",) if f in OUTER_TILES else ("wr", "wj"):
                for g in range(PASSES):
                    multiply_part(c, f, weight, g)

        def clip(x, c, f):
            receivers = slice(c * CHUNK_RECEIVERS, (c + 1) * CHUNK_RECEIVERS)
            clipped = clip_pool.tile([P, CHUNK_RECEIVERS, NODES], F32)
            nc.vector.tensor_tensor(
                out=clipped[:],
                in0=x,
                in1=thresholds[(c, f)][:]
                if f in OUTER_TILES
                else neg_recv[:, f, receivers]
                .unsqueeze(2)
                .to_broadcast([P, CHUNK_RECEIVERS, NODES]),
                op=MAX,
            )
            return clipped, sums[:, f, receivers]

        def fold(clipped):
            folded = clip_pool.tile([P, CHUNK_RECEIVERS, NODES // 2], F32)
            nc.gpsimd.tensor_tensor(
                out=folded[:],
                in0=clipped[:, :, 0 : NODES // 2],
                in1=clipped[:, :, NODES // 2 : NODES],
                op=ADD,
            )
            return folded

        def sum_bank(folded, target):
            nc.vector.tensor_reduce(out=target, in_=folded[:], axis=mybir.AxisListType.X, op=ADD)

        def scalar_sums(x, c, f):
            junk = junk_pool.tile([P, CHUNK_RECEIVERS, NODES], F32)
            for i in range(CHUNK_RECEIVERS):
                r = c * CHUNK_RECEIVERS + i
                nc.scalar.activation(
                    out=junk[:, i, :],
                    in_=x[:, i, :],
                    func=RELU,
                    bias=scalar_recv[:, f, r : r + 1],
                    accum_out=sums[:, f, r : r + 1],
                )

        waiting = []

        def drain_bank(c, f, folded=True):
            x = x_acc[(c, f)][:].rearrange("p (i j) -> p i j", j=NODES)
            if f in SCALAR_TILES and not (f == EARLY_TILE and c < EARLY_CHUNKS):
                scalar_sums(x, c, f)
                return
            clipped, target = clip(x, c, f)
            waiting.append((fold(clipped) if folded and f != 3 else clipped, target))

        def sum_waiting(keep_back):
            while len(waiting) > keep_back:
                sum_bank(*waiting.pop(0))

        agg_bf = const.tile([P, PASSES, P, PACK], BF16, align_bytes=64)
        agg_codes = const.tile([P, PASSES, P], U32, align_bytes=64)
        agg_scales = const.tile([P, PASSES, P], U8, align_bytes=64)

        def aggregate(g):
            tiles = slice(PACK * g, PACK * (g + 1))
            nc.vector.scalar_tensor_tensor(
                out=agg_bf[:, g],
                in0=neg_recv[:, tiles, :].rearrange("p t r -> p r t"),
                scalar=-float(NODES),
                in1=sums[:, tiles, :].rearrange("p t r -> p r t"),
                op0=MULT,
                op1=ADD,
            )
            nc.vector.quantize_mx(
                out=agg_codes[:, g, :].bitcast(FP8X4),
                scales=agg_scales[:, g, :],
                in_=agg_bf[:, g].rearrange("p r t -> p (r t)"),
            )


        def transpose_chunk(c, half):
            transpose_banks(c, 2 * half, 2 * half + 2)
            copy_banks(c, 2 * half, 2 * half + 2)

        def prepare_pass(weight, g, by_vector):
            for quarter in range(QUARTERS):
                regroup(weight, quarter, g, "vector" if quarter < by_vector else "scalar")

        def quantise_pass(weight, g):
            for quarter in range(QUARTERS):
                quantise(weight, quarter, g)

        prepare_pass("wr", 0, 3)
        transpose_chunk(0, 0)
        transpose_chunk(0, 1)
        quantise_pass("wr", 0)
        prepare_pass("wr", 1, 3)
        prepare_particles()
        quantise_chunk(0, 0)
        quantise_chunk(0, 1)
        prepare_bias()
        for f in range(OPEN):
            multiply_part(0, f, "wr", 0)
        quantise_pass("wr", 1)
        prepare_pass("wj", 0, 2)
        repeat_senders(0)
        for f in range(OPEN):
            multiply_part(0, f, "wr", 1)
        quantise_pass("wj", 0)
        prepare_pass("wj", 1, 2)
        for f in range(OPEN):
            if f not in OUTER_TILES:
                multiply_part(0, f, "wj", 0)
        quantise_pass("wj", 1)
        prepare_pass("wi", 0, 2)
        for f in range(OPEN):
            if f not in OUTER_TILES:
                multiply_part(0, f, "wj", 1)
        for f in OUTER_TILES:
            sender_terms(f)
        quantise_pass("wi", 0)
        prepare_pass("wi", 1, 2)
        transpose_chunk(1, 0)
        quantise_pass("wi", 1)
        transpose_chunk(1, 1)
        for quarter in range(QUARTERS):
            multiply_receivers(quarter)
            receiver_terms(quarter)
        for f in OUTER_TILES:
            make_threshold(0, f)
        quantise_chunk(1, 0)
        quantise_chunk(1, 1)

        late = [(weight, g) for weight in ("po", "pa") for g in range(PASSES)]
        late_pieces = [(weight, quarter, g) for weight, g in late for quarter in range(QUARTERS)]
        slot = 0
        for c in range(CHUNKS):
            for f in range(F_TILES):
                if c > 0 or f >= OPEN:
                    multiply_bank(c, f)
                last = c == CHUNKS - 1 and f == F_TILES - 1
                drain_bank(c, f, folded=not last)
                if f in OUTER_TILES and c + 1 < CHUNKS:
                    make_threshold(c + 1, f)
                if c == 1 and f in OUTER_TILES:
                    outer_means(f)
                if slot == 0:
                    load_chunk(2)
                if slot % 12 == 8 and slot // 12 < len(late):
                    load_weight(*late[slot // 12])
                n = slot - 14
                if n >= 0 and n // 3 < len(late_pieces):
                    if n % 3 == 0:
                        regroup(*late_pieces[n // 3], "vector")
                    if n % 3 == 1:
                        quantise(*late_pieces[n // 3])
                if 0 < c < CHUNKS - 1:
                    if f == 1:
                        quantise_chunk(c + 1, 0)
                    if f == 3:
                        quantise_chunk(c + 1, 1)
                if c < CHUNKS - 1:
                    if f == 6 and (c + 1) * CHUNK_RECEIVERS % NODES == 0:
                        repeat_senders((c + 1) * CHUNK_RECEIVERS // NODES)
                if c + 2 < CHUNKS:
                    if f == 0 and c > 0:
                        load_chunk(c + 2)
                    if f == (7 if c == 0 else 5):
                        transpose_chunk(c + 2, 0)
                    if f == 7 and c > 0:
                        transpose_chunk(c + 2, 1)
                if c == 1 and f == 1:
                    transpose_chunk(2, 1)
                if c == CHUNKS - 1 and f == F_TILES - 3:
                    sum_waiting(1)
                    aggregate(0)
                sum_waiting(0 if last else SUM_LAG)
                slot += 1
        pp_bias = const.tile([P, NF], BF16)
        nc.sync.dma_start(out=pp_bias[:], in_=pp_b.partition_broadcast(P))

        totals = []
        for h in range(HALVES):
            total = psum_e.tile([P, BANK], F32, tag="acc")
            totals.append(total)
        products = (
            ("po", obj_codes, obj_scales, 0),
            ("po", obj_codes, obj_scales, 1),
            ("pa", agg_codes, agg_scales, 0),
            ("pa", agg_codes, agg_scales, 1),
        )

        def last_product(h, n):
            weight, codes, scales, g = products[n]
            cols = slice(BANK * h, BANK * (h + 1))
            nc.tensor.matmul_mx(
                out=totals[h][:],
                lhsT=codes[:, g, :].bitcast(FP8X4),
                lhsT_scale=scales[:, g, :],
                rhs=w_codes[weight][:, g, cols].bitcast(FP8X4),
                rhs_scale=w_scales[weight][:, g, cols],
                start=(n == 0),
                stop=(n == len(products) - 1),
            )

        for h in range(HALVES):
            for n in range(len(products) - 1):
                last_product(h, n)
        aggregate(1)
        for h in range(HALVES):
            last_product(h, len(products) - 1)
        for h in range(HALVES):
            for part in range(2):
                here = slice(QW * part, QW * (part + 1))
                cols = slice(BANK * h + QW * part, BANK * h + QW * (part + 1))
                result = result_pool.tile([P, QW], F32)
                nc.vector.tensor_tensor(
                    out=result[:], in0=totals[h][:, here], in1=pp_bias[:, cols], op=ADD
                )
                nc.scalar.activation(out=result[:], in_=result[:], func=RELU)
                nc.sync.dma_start(out=out_rows[:, cols], in_=result[:])
